import numpy as np
import ml_dtypes


def mxq(x, axis, fmt="e4m3"):
    dtype, down = {"e4m3": (ml_dtypes.float8_e4m3fn, 7), "e5m2": (ml_dtypes.float8_e5m2, 14)}[fmt]
    v = np.moveaxis(np.asarray(x, np.float32).astype(ml_dtypes.bfloat16).astype(np.float64), axis, -1)
    blocks = v.reshape(v.shape[:-1] + (-1, 32))
    amax = np.abs(blocks).max(-1, keepdims=True)
    byte = np.maximum(np.where(amax > 0, np.frexp(amax)[1] - 1 + 127, 0) - down, 1)
    scale = np.exp2(byte - 127.0)
    codes = (blocks / scale).astype(np.float32).astype(dtype).astype(np.float64)
    return np.moveaxis((codes * scale).reshape(v.shape), -1, axis)


WIDE = False


def mx_kscale(k):
    if not WIDE:
        return np.ones(k)
    levels = np.array([10, -10, 5, -5, 0])
    a = np.random.permutation(np.resize(levels, k // 512 * 4)).reshape(k // 512, 4)
    idx = np.arange(k)
    return np.exp2(a[idx // 512, idx % 128 // 32])


BF16 = ml_dtypes.bfloat16


def bf(x):
    return np.asarray(x, np.float32).astype(BF16)


def f64(x):
    return np.asarray(x).astype(np.float64)


B, RES, C, NH, RD, RW = 32, 16, 1024, 8, 32, 128
N, L = B * RES, RES
KG = L * RD


def setup_inputs():
    s = mx_kscale(C)
    return {"x_seq": bf(np.random.standard_normal((N, L, C)) * s),
            "Wc": bf(np.random.standard_normal((NH * RD, C)) / np.sqrt(C) / s),
            "bc": bf(np.random.standard_normal(NH * RD) * 0.3),
            "Wg": bf(np.random.standard_normal((L * L, KG)) * 1.5 / np.sqrt(KG)),
            "bg": bf(np.random.standard_normal(L * L) * 0.5)}


def reference(x_seq, Wc, bc, Wg, bg):
    w = (mxq(f64(x_seq), 2, "e4m3") @ mxq(f64(Wc), 1, "e4m3").T) + f64(bc)
    w = w.reshape(N, L, NH, RD).transpose(0, 2, 1, 3).reshape(N, NH, KG)
    w = ((mxq(w, 2, "e4m3") @ mxq(f64(Wg), 1, "e4m3").T) + f64(bg)).reshape(N, NH, L, L)
    e = np.exp(w - w.max(-2, keepdims=True))
    return e / e.sum(-2, keepdims=True)

@@ -1,0 +1,272 @@
+from contextlib import ExitStack
+
+import concourse.mybir as mybir
+from concourse.masks import make_identity
+
+F32 = mybir.dt.float32
+BF16 = mybir.dt.bfloat16
+U32 = mybir.dt.uint32
+U8 = mybir.dt.uint8
+I32 = mybir.dt.int32
+FP8X4 = mybir.dt.float8_e4m3fn_x4
+ALU = mybir.AluOpType
+ACTF = mybir.ActivationFunctionType
+AX = mybir.AxisListType
+
+P = 128
+FLOPS = 2 * 8192 * 1024 * 256 + 2 * 4096 * 512 * 256
+
+N_UNITS = 16
+N_BANKS = 16
+PREFETCH = 3
+
+
+def tile_dynamixerblock_pa_t_kernel(tc, x_seq, Wc, bc, Wg, bg, out):
+    nc = tc.nc
+    out_rows = out.rearrange("(a p) h i j -> a p (h i j)", p=P)
+    with ExitStack() as ctx:
+        const = ctx.enter_context(tc.tile_pool(name="const", bufs=1))
+        xin = ctx.enter_context(tc.tile_pool(name="xin", bufs=5))
+        xgp = ctx.enter_context(tc.tile_pool(name="xgp", bufs=2))
+        xwp = ctx.enter_context(tc.tile_pool(name="xwp", bufs=3))
+        vgp = ctx.enter_context(tc.tile_pool(name="vgp", bufs=3))
+        vwp = ctx.enter_context(tc.tile_pool(name="vwp", bufs=2))
+        smp = ctx.enter_context(tc.tile_pool(name="smp", bufs=3))
+        ps_t = ctx.enter_context(tc.psum_pool(name="ps_t", bufs=4))
+        ps_1 = ctx.enter_context(tc.psum_pool(name="ps_1", bufs=2))
+        ps_2 = ctx.enter_context(tc.psum_pool(name="ps_2", bufs=2))
+        ctx.enter_context(tc.manual_schedule())
+
+        xs_of = {}
+        bank_of = {}
+        xw_of = {}
+        acc1_of = {}
+        vw_of = {}
+        acc2_of = {}
+        sm_of = {}
+
+        wc_sb = const.tile([P, 2, 1024], BF16, tag="wc_sb")
+        nc.sync.dma_start(out=wc_sb[:], in_=Wc.rearrange("(h p) k -> p h k", p=P))
+        wg_sb = const.tile([P, 2, 512], BF16, tag="wg_sb")
+        nc.scalar.dma_start(out=wg_sb[:], in_=Wg.rearrange("(a p) k -> p a k", p=P))
+        bc_b = const.tile([P, 2], BF16, tag="bc_b")
+        with nc.allow_non_contiguous_dma(reason="256 bias values, one per partition"):
+            nc.scalar.dma_start(out=bc_b[:], in_=bc.rearrange("(h p) -> p h", p=P))
+        bg_b = const.tile([P, 256], BF16, tag="bg_b")
+        nc.scalar.dma_start(out=bg_b[:], in_=bg.partition_broadcast(P))
+
+        def load(k):
+            nt, lg = divmod(k, 4)
+            xs = xin.tile([P, 4, 1024], BF16, tag="xs")
+            nc.sync.dma_start(out=xs[:], in_=x_seq[nt * P:(nt + 1) * P, 4 * lg:4 * lg + 4, :])
+            xs_of[k] = xs
+
+        for k in range(PREFETCH):
+            load(k)
+
+        ident_f = const.tile([P, P], F32, tag="ident_f")
+        make_identity(nc, ident_f[:])
+        ident_b = const.tile([P, P], BF16, tag="ident_b")
+        make_identity(nc, ident_b[:])
+
+        wbd = const.tile([P, 4, 1024], U32, tag="wbd", align_bytes=64)
+        wbds = const.tile([P, 4, 1024], U8, tag="wbds", align_bytes=64)
+        nc.vector.memset(wbd[:].bitcast(I32), 0)
+        nc.vector.memset(wbds[:].bitcast(I32), 0)
+
+        bct = const.tile([P, 2], F32, tag="bct")
+        nc.vector.tensor_copy(out=bct[:], in_=bc_b[:])
+        bgb = const.tile([P, 256], F32, tag="bgb")
+        nc.vector.tensor_copy(out=bgb[:], in_=bg_b[:])
+
+        wcg = const.tile([P, 2048], BF16, tag="wcg", align_bytes=64)
+        wcg32 = wcg[:].bitcast(F32).rearrange("p (g h m u) -> p g h m u", g=2, h=2, m=P, u=2)
+        wc32 = wc_sb[:].bitcast(F32)
+        for hh in range(2):
+            wbank = ps_t.tile([P, 4, P], F32, tag="xt")
+            for c in range(4):
+                nc.tensor.transpose(wbank[:, c, :], wc32[:, hh, c * P:(c + 1) * P], ident_f[:])
+            nc.scalar.copy(out=wcg32[:, :, hh, :, :],
+                           in_=wbank[:].rearrange("p (g u) m -> p g m u", g=2))
+        wcw = const.tile([P, 512], U32, tag="wcw", align_bytes=64)
+        wcs = const.tile([P, 512], U8, tag="wcs", align_bytes=64)
+        nc.vector.quantize_mx(out=wcw[:].bitcast(FP8X4), scales=wcs[:], in_=wcg[:])
+
+        wdup = const.tile([P, 2, 16, P], BF16, tag="wdup")
+        nc.vector.tensor_copy(
+            out=wdup[:].rearrange("p a l (d r) -> p (a l) d r", d=4),
+            in_=wg_sb[:].rearrange("p a (l r) -> p (a l) r", r=32).unsqueeze(2).to_broadcast([P, 32, 4, 32]))
+        wgg = const.tile([P, 4, 256, 4], BF16, tag="wgg", align_bytes=64)
+        wgw = const.tile([P, 4, 256], U32, tag="wgw", align_bytes=64)
+        wgs = const.tile([P, 4, 256], U8, tag="wgs", align_bytes=64)
+
+        def wg_transposes(lg):
+            wgp = ps_2.tile([P, 4, 256], BF16, tag="s2")
+            for t in range(4):
+                for a in range(2):
+                    nc.tensor.transpose(wgp[:, t, a * P:(a + 1) * P], wdup[:, a, 4 * lg + t, :], ident_b[:])
+            return wgp
+
+        def wg_regroup(lg, wgp):
+            nc.vector.tensor_copy(out=wgg[:, lg, :, :], in_=wgp[:].rearrange("p t c -> p c t"))
+
+        def wg_finish():
+            nc.vector.quantize_mx(out=wgw[:].rearrange("p a c -> p (a c)").bitcast(FP8X4),
+                                  scales=wgs[:].rearrange("p a c -> p (a c)"),
+                                  in_=wgg[:].rearrange("p a c t -> p (a c t)"))
+            for d in range(4):
+                nc.vector.tensor_copy(out=wbd[32 * d:32 * d + 32, :, 256 * d:256 * d + 256].bitcast(I32),
+                                      in_=wgw[32 * d:32 * d + 32, :, :].bitcast(I32))
+                nc.vector.tensor_copy(out=wbds[32 * d:32 * d + 4, :, 256 * d:256 * d + 256].bitcast(I32),
+                                      in_=wgs[32 * d:32 * d + 4, :, :].bitcast(I32))
+
+        def transposes(k):
+            xs32 = xs_of[k][:].bitcast(F32)
+            banks = []
+            for t in range(4):
+                bank = ps_t.tile([P, 4, P], F32, tag="xt")
+                for c in range(4):
+                    nc.tensor.transpose(bank[:, c, :], xs32[:, t, c * P:(c + 1) * P], ident_f[:])
+                banks.append(bank)
+            bank_of[k] = banks
+
+        def regroup(k):
+            xg = xgp.tile([P, 4096], BF16, tag="xg", align_bytes=64)
+            xg32 = xg[:].bitcast(F32).rearrange("p (g t n u) -> p g t n u", g=2, t=4, n=P, u=2)
+            for t in range(4):
+                src = bank_of[k][t][:].rearrange("p (g u) n -> p g n u", g=2)
+                if t < 3:
+                    nc.scalar.copy(out=xg32[:, :, t, :, :], in_=src)
+                else:
+                    nc.vector.tensor_copy(out=xg32[:, :, t, :, :], in_=src)
+            return xg
+
+        def quantise_x(k, xg):
+            xw = xwp.tile([P, 1024], U32, tag="xw", align_bytes=64)
+            xsc = xwp.tile([P, 1024], U8, tag="xsc", align_bytes=64)
+            nc.vector.quantize_mx(out=xw[:].bitcast(FP8X4), scales=xsc[:], in_=xg[:])
+            xw_of[k] = (xw, xsc)
+
+        def stage1(k):
+            xw, xsc = xw_of[k]
+            accs = []
+            for hh in range(2):
+                acc = ps_1.tile([P, 512], F32, tag="s1")
+                for g in range(2):
+                    w0 = (g * 2 + hh) * P
+                    nc.tensor.matmul_mx(out=acc[:],
+                                        lhsT=wcw[:, w0:w0 + P].bitcast(FP8X4), lhsT_scale=wcs[:, w0:w0 + P],
+                                        rhs=xw[:, g * 512:(g + 1) * 512].bitcast(FP8X4),
+                                        rhs_scale=xsc[:, g * 512:(g + 1) * 512],
+                                        start=(g == 0), stop=(g == 1))
+                accs.append(acc)
+            acc1_of[k] = accs
+
+        def bias_round(k):
+            vg = vgp.tile([P, 2, P, 4], BF16, tag="vg", align_bytes=64)
+            for hh in range(2):
+                nc.scalar.activation(out=vg[:, hh, :, :],
+                                     in_=acc1_of[k][hh][:].rearrange("p (t n) -> p n t", t=4),
+                                     func=ACTF.Identity, bias=bct[:, hh:hh + 1], scale=1.0)
+            return vg
+
+        def quantise_v(k, vg):
+            nt, lg = divmod(k, 4)
+            if lg == 0:
+                vw = vwp.tile([P, 4, 256], U32, tag="vw", align_bytes=64)
+                vsc = vwp.tile([P, 4, 256], U8, tag="vsc", align_bytes=64)
+                vw_of[nt] = (vw, vsc)
+            vw, vsc = vw_of[nt]
+            nc.vector.quantize_mx(out=vw[:, lg, :].bitcast(FP8X4), scales=vsc[:, lg, :],
+                                  in_=vg[:].rearrange("p h n t -> p (h n t)"))
+
+        def stage2(b):
+            nt, r = divmod(b, 4)
+            hh, half = divmod(r, 2)
+            vw, vsc = vw_of[nt]
+            acc2 = ps_2.tile([P, 512], F32, tag="s2")
+            for lg in range(4):
+                nc.tensor.matmul_mx(out=acc2[:],
+                                    lhsT=vw[:, lg, hh * P:(hh + 1) * P].bitcast(FP8X4),
+                                    lhsT_scale=vsc[:, lg, hh * P:(hh + 1) * P],
+                                    rhs=wbd[:, lg, half * 512:(half + 1) * 512].bitcast(FP8X4),
+                                    rhs_scale=wbds[:, lg, half * 512:(half + 1) * 512],
+                                    start=(lg == 0), stop=(lg == 3))
+            acc2_of[b] = acc2
+
+        def by_hij(ap):
+            return ap.rearrange("p (h i j) -> p h i j", h=2, i=16, j=16)
+
+        def by_hji(ap):
+            return ap.rearrange("p (h i j) -> p h j i", h=2, i=16, j=16)
+
+        def over_i(small):
+            return small[:].unsqueeze(2).to_broadcast([P, 2, 16, 16])
+
+        def soft_a(b):
+            tt = smp.tile([P, 512], F32, tag="tt")
+            nc.vector.tensor_tensor(out=tt[:].rearrange("p (h c) -> p h c", h=2),
+                                    in0=acc2_of[b][:].rearrange("p (h c) -> p h c", h=2),
+                                    in1=bgb[:].unsqueeze(1).to_broadcast([P, 2, 256]), op=ALU.add)
+            mx = smp.tile([P, 2, 16], F32, tag="mx")
+            nc.vector.tensor_reduce(out=mx[:], in_=by_hji(tt[:]), axis=AX.X, op=ALU.max)
+            sm_of[b] = [tt, mx]
+
+        def soft_b_sub(b):
+            tt, mx = sm_of[b]
+            dd = smp.tile([P, 512], F32, tag="dd")
+            nc.gpsimd.tensor_tensor(out=by_hij(dd[:]), in0=by_hij(tt[:]), in1=over_i(mx), op=ALU.subtract)
+            sm_of[b] = [dd]
+
+        def soft_b_exp(b):
+            dd = sm_of[b][0]
+            nc.scalar.activation(out=dd[:], in_=dd[:], func=ACTF.Exp)
+
+        def soft_c_sum(b):
+            dd = sm_of[b][0]
+            sm = smp.tile([P, 2, 16], F32, tag="sm")
+            nc.vector.tensor_reduce(out=sm[:], in_=by_hji(dd[:]), axis=AX.X, op=ALU.add)
+            rs = smp.tile([P, 2, 16], F32, tag="rs")
+            nc.vector.reciprocal(out=rs[:], in_=sm[:])
+            sm_of[b] = [dd, rs]
+
+        def soft_c_norm(b):
+            dd, rs = sm_of[b]
+            oo = smp.tile([P, 512], F32, tag="oo")
+            nc.gpsimd.tensor_tensor(out=by_hij(oo[:]), in0=by_hij(dd[:]), in1=over_i(rs), op=ALU.mult)
+            nt, r = divmod(b, 4)
+            nc.sync.dma_start(out=out_rows[nt][:, r * 512:(r + 1) * 512], in_=oo[:])
+
+        def has(i, n):
+            return 0 <= i < n
+
+        for q in range(-1, N_BANKS + 8):
+            if has(q + PREFETCH, N_UNITS) and q + PREFETCH >= PREFETCH:
+                load(q + PREFETCH)
+            if has(q + 1, N_UNITS):
+                transposes(q + 1)
+            wgp = wg_transposes(q) if has(q, 4) else None
+            if has(q - 7, N_BANKS):
+                soft_c_sum(q - 7)
+            if has(q - 6, N_BANKS):
+                soft_b_sub(q - 6)
+            if has(q - 7, N_BANKS):
+                soft_c_norm(q - 7)
+            if has(q - 5, N_BANKS):
+                soft_a(q - 5)
+            xg = regroup(q + 1) if has(q + 1, N_UNITS) else None
+            if has(q, N_UNITS):
+                stage1(q)
+            if has(q - 4, N_BANKS):
+                stage2(q - 4)
+            vg = bias_round(q) if has(q, N_UNITS) else None
+            if wgp is not None:
+                wg_regroup(q, wgp)
+            if xg is not None:
+                quantise_x(q + 1, xg)
+            if has(q - 6, N_BANKS):
+                soft_b_exp(q - 6)
+            if vg is not None:
+                quantise_v(q, vg)
+            if q == 3:
+                wg_finish()

@@ -77,7 +77,8 @@ def tile_dynamixerblock_pa_t_kernel(tc, x_seq, Wc, bc, Wg, bg, out):
         bct = const.tile([P, 2], F32, tag="bct")
         nc.vector.tensor_copy(out=bct[:], in_=bc_b[:])
         bgb = const.tile([P, 256], F32, tag="bgb")
-        nc.vector.tensor_copy(out=bgb[:], in_=bg_b[:])
+        nc.vector.tensor_copy(out=bgb[:].rearrange("p (a i b) -> p a i b", a=8, i=16, b=2),
+                              in_=bg_b[:].rearrange("p (i a b) -> p a i b", a=8, i=16, b=2))
 
         wcg = const.tile([P, 2048], BF16, tag="wcg", align_bytes=64)
         wcg32 = wcg[:].bitcast(F32).rearrange("p (g h m u) -> p g h m u", g=2, h=2, m=P, u=2)
@@ -108,7 +109,8 @@ def tile_dynamixerblock_pa_t_kernel(tc, x_seq, Wc, bc, Wg, bg, out):
             return wgp
 
         def wg_regroup(lg, wgp):
-            nc.vector.tensor_copy(out=wgg[:, lg, :, :], in_=wgp[:].rearrange("p t c -> p c t"))
+            nc.vector.tensor_copy(out=wgg[:, lg, :, :].rearrange("p (a i b) t -> p a i b t", a=8, i=16, b=2),
+                                  in_=wgp[:].rearrange("p t (i a b) -> p a i b t", a=8, i=16, b=2))
 
         def wg_finish():
             nc.vector.quantize_mx(out=wgw[:].rearrange("p a c -> p (a c)").bitcast(FP8X4),
@@ -194,67 +196,74 @@ def tile_dynamixerblock_pa_t_kernel(tc, x_seq, Wc, bc, Wg, bg, out):
                                     start=(lg == 0), stop=(lg == 3))
             acc2_of[b] = acc2
 
-        def by_hij(ap):
-            return ap.rearrange("p (h i j) -> p h i j", h=2, i=16, j=16)
+        def by_aib(ap):
+            return ap.rearrange("p (a i b) -> p a i b", a=16, i=16, b=2)
 
-        def by_hji(ap):
-            return ap.rearrange("p (h i j) -> p h j i", h=2, i=16, j=16)
+        def by_abi(ap):
+            return ap.rearrange("p (a i b) -> p a b i", a=16, i=16, b=2)
 
-        def over_i(small):
-            return small[:].unsqueeze(2).to_broadcast([P, 2, 16, 16])
-
-        def soft_a(b):
-            tt = smp.tile([P, 512], F32, tag="tt")
+        def soft_bias_max(b):
+            tt = smp.tile([P, 512], F32, tag="tt", bufs=2)
             nc.vector.tensor_tensor(out=tt[:].rearrange("p (h c) -> p h c", h=2),
                                     in0=acc2_of[b][:].rearrange("p (h c) -> p h c", h=2),
                                     in1=bgb[:].unsqueeze(1).to_broadcast([P, 2, 256]), op=ALU.add)
-            mx = smp.tile([P, 2, 16], F32, tag="mx")
-            nc.vector.tensor_reduce(out=mx[:], in_=by_hji(tt[:]), axis=AX.X, op=ALU.max)
+            mx = smp.tile([P, 16, 2], F32, tag="mx", bufs=2)
+            nc.vector.tensor_reduce(out=mx[:], in_=by_abi(tt[:]), axis=AX.X, op=ALU.max)
             sm_of[b] = [tt, mx]
 
-        def soft_b_sub(b):
+        def soft_sub(b):
             tt, mx = sm_of[b]
-            dd = smp.tile([P, 512], F32, tag="dd")
-            nc.gpsimd.tensor_tensor(out=by_hij(dd[:]), in0=by_hij(tt[:]), in1=over_i(mx), op=ALU.subtract)
+            dd = smp.tile([P, 512], F32, tag="dd", bufs=4)
+            nc.gpsimd.tensor_tensor(out=by_aib(dd[:]), in0=by_aib(tt[:]),
+                                    in1=mx[:].unsqueeze(2).to_broadcast([P, 16, 16, 2]), op=ALU.subtract)
             sm_of[b] = [dd]
 
-        def soft_b_exp(b):
+        def soft_exp(b):
             dd = sm_of[b][0]
             nc.scalar.activation(out=dd[:], in_=dd[:], func=ACTF.Exp)
 
-        def soft_c_sum(b):
+        def soft_sum(b):
             dd = sm_of[b][0]
-            sm = smp.tile([P, 2, 16], F32, tag="sm")
-            nc.vector.tensor_reduce(out=sm[:], in_=by_hji(dd[:]), axis=AX.X, op=ALU.add)
-            rs = smp.tile([P, 2, 16], F32, tag="rs")
-            nc.vector.reciprocal(out=rs[:], in_=sm[:])
+            sm = smp.tile([P, 16, 2], F32, tag="sm", bufs=2)
+            nc.vector.tensor_reduce(out=sm[:], in_=by_abi(dd[:]), axis=AX.X, op=ALU.add)
+            sm_of[b] = [dd, sm]
+
+        def soft_recip(b):
+            dd, sm = sm_of[b]
+            rs = smp.tile([P, 2, 16], F32, tag="rs", bufs=3)
+            nc.vector.reciprocal(out=rs[:].rearrange("p h j -> p (h j)"), in_=sm[:].rearrange("p a b -> p (a b)"))
             sm_of[b] = [dd, rs]
 
-        def soft_c_norm(b):
+        def soft_norm_store(b):
             dd, rs = sm_of[b]
-            oo = smp.tile([P, 512], F32, tag="oo")
-            nc.gpsimd.tensor_tensor(out=by_hij(oo[:]), in0=by_hij(dd[:]), in1=over_i(rs), op=ALU.mult)
+            oo = smp.tile([P, 2, 16, 16], F32, tag="oo", bufs=3)
+            for h in range(2):
+                nc.gpsimd.tensor_tensor(
+                    out=oo[:, h, :, :].rearrange("p i (a b) -> p i a b", b=2),
+                    in0=dd[:, h * 256:(h + 1) * 256].rearrange("p (a i b) -> p i a b", a=8, i=16, b=2),
+                    in1=rs[:, h, :].rearrange("p (a b) -> p a b", b=2).unsqueeze(1).to_broadcast([P, 16, 8, 2]),
+                    op=ALU.mult)
             nt, r = divmod(b, 4)
-            nc.sync.dma_start(out=out_rows[nt][:, r * 512:(r + 1) * 512], in_=oo[:])
+            nc.sync.dma_start(out=out_rows[nt][:, r * 512:(r + 1) * 512],
+                              in_=oo[:].rearrange("p h i j -> p (h i j)"))
 
         def has(i, n):
             return 0 <= i < n
 
         for q in range(-1, N_BANKS + 8):
-            if has(q + PREFETCH, N_UNITS) and q + PREFETCH >= PREFETCH:
+            if has(q + PREFETCH, N_UNITS) and q >= 0:
                 load(q + PREFETCH)
             if has(q + 1, N_UNITS):
                 transposes(q + 1)
             wgp = wg_transposes(q) if has(q, 4) else None
             if has(q - 7, N_BANKS):
-                soft_c_sum(q - 7)
-            if has(q - 6, N_BANKS):
-                soft_b_sub(q - 6)
-            if has(q - 7, N_BANKS):
-                soft_c_norm(q - 7)
+                soft_norm_store(q - 7)
             if has(q - 5, N_BANKS):
-                soft_a(q - 5)
+                soft_bias_max(q - 5)
+                soft_sub(q - 5)
             xg = regroup(q + 1) if has(q + 1, N_UNITS) else None
+            if has(q - 6, N_BANKS):
+                soft_sum(q - 6)
             if has(q, N_UNITS):
                 stage1(q)
             if has(q - 4, N_BANKS):
@@ -264,9 +273,11 @@ def tile_dynamixerblock_pa_t_kernel(tc, x_seq, Wc, bc, Wg, bg, out):
                 wg_regroup(q, wgp)
             if xg is not None:
                 quantise_x(q + 1, xg)
-            if has(q - 6, N_BANKS):
-                soft_b_exp(q - 6)
+            if has(q - 5, N_BANKS):
+                soft_exp(q - 5)
             if vg is not None:
                 quantise_v(q, vg)
+            if has(q - 6, N_BANKS):
+                soft_recip(q - 6)
             if q == 3:
                 wg_finish()

@@ -23,14 +23,15 @@ PREFETCH = 3
 
 def tile_dynamixerblock_pa_t_kernel(tc, x_seq, Wc, bc, Wg, bg, out):
     nc = tc.nc
-    out_rows = out.rearrange("(a p) h i j -> a p (h i j)", p=P)
+    x_rows = x_seq.rearrange("n (a b) c -> (n a) b c", a=2)
+    out_rows = out.rearrange("(g n) (hh q) i j -> g hh n (q i j)", n=64, hh=2)
     with ExitStack() as ctx:
         const = ctx.enter_context(tc.tile_pool(name="const", bufs=1))
         xin = ctx.enter_context(tc.tile_pool(name="xin", bufs=5))
         xgp = ctx.enter_context(tc.tile_pool(name="xgp", bufs=2))
         xwp = ctx.enter_context(tc.tile_pool(name="xwp", bufs=3))
         vgp = ctx.enter_context(tc.tile_pool(name="vgp", bufs=3))
-        vwp = ctx.enter_context(tc.tile_pool(name="vwp", bufs=2))
+        vwp = ctx.enter_context(tc.tile_pool(name="vwp", bufs=3))
         smp = ctx.enter_context(tc.tile_pool(name="smp", bufs=3))
         ps_t = ctx.enter_context(tc.psum_pool(name="ps_t", bufs=4))
         ps_1 = ctx.enter_context(tc.psum_pool(name="ps_1", bufs=2))
@@ -44,6 +45,7 @@ def tile_dynamixerblock_pa_t_kernel(tc, x_seq, Wc, bc, Wg, bg, out):
         vw_of = {}
         acc2_of = {}
         sm_of = {}
+        wgp_of = {}
 
         wc_sb = const.tile([P, 2, 1024], BF16, tag="wc_sb")
         nc.sync.dma_start(out=wc_sb[:], in_=Wc.rearrange("(h p) k -> p h k", p=P))
@@ -56,9 +58,9 @@ def tile_dynamixerblock_pa_t_kernel(tc, x_seq, Wc, bc, Wg, bg, out):
         nc.scalar.dma_start(out=bg_b[:], in_=bg.partition_broadcast(P))
 
         def load(k):
-            nt, lg = divmod(k, 4)
+            ng, bq = divmod(k, 2)
             xs = xin.tile([P, 4, 1024], BF16, tag="xs")
-            nc.sync.dma_start(out=xs[:], in_=x_seq[nt * P:(nt + 1) * P, 4 * lg:4 * lg + 4, :])
+            nc.sync.dma_start(out=xs[:], in_=x_rows[ng * P:(ng + 1) * P, 4 * bq:4 * bq + 4, :])
             xs_of[k] = xs
 
         for k in range(PREFETCH):
@@ -73,6 +75,9 @@ def tile_dynamixerblock_pa_t_kernel(tc, x_seq, Wc, bc, Wg, bg, out):
         wbds = const.tile([P, 4, 1024], U8, tag="wbds", align_bytes=64)
         nc.vector.memset(wbd[:].bitcast(I32), 0)
         nc.vector.memset(wbds[:].bitcast(I32), 0)
+        perm_f = const.tile([P, P], F32, tag="perm_f")
+        nc.vector.tensor_copy(out=perm_f[:].rearrange("p (a n) -> p a n", a=2),
+                              in_=ident_f[:].rearrange("p (n a) -> p a n", a=2))
 
         bct = const.tile([P, 2], F32, tag="bct")
         nc.vector.tensor_copy(out=bct[:], in_=bc_b[:])
@@ -94,33 +99,38 @@ def tile_dynamixerblock_pa_t_kernel(tc, x_seq, Wc, bc, Wg, bg, out):
         nc.vector.quantize_mx(out=wcw[:].bitcast(FP8X4), scales=wcs[:], in_=wcg[:])
 
         wdup = const.tile([P, 2, 16, P], BF16, tag="wdup")
-        nc.vector.tensor_copy(
+        nc.gpsimd.tensor_scalar(
             out=wdup[:].rearrange("p a l (d r) -> p (a l) d r", d=4),
-            in_=wg_sb[:].rearrange("p a (l r) -> p (a l) r", r=32).unsqueeze(2).to_broadcast([P, 32, 4, 32]))
+            in0=wg_sb[:].rearrange("p a (l r) -> p (a l) r", r=32).unsqueeze(2).to_broadcast([P, 32, 4, 32]),
+            scalar1=1.0, scalar2=0.0, op0=ALU.mult, op1=ALU.add)
         wgg = const.tile([P, 4, 256, 4], BF16, tag="wgg", align_bytes=64)
         wgw = const.tile([P, 4, 256], U32, tag="wgw", align_bytes=64)
         wgs = const.tile([P, 4, 256], U8, tag="wgs", align_bytes=64)
 
-        def wg_transposes(lg):
-            wgp = ps_2.tile([P, 4, 256], BF16, tag="s2")
-            for t in range(4):
-                for a in range(2):
-                    nc.tensor.transpose(wgp[:, t, a * P:(a + 1) * P], wdup[:, a, 4 * lg + t, :], ident_b[:])
-            return wgp
+        def wg_transposes(pair):
+            for lg in (2 * pair, 2 * pair + 1):
+                wgp = ps_2.tile([P, 4, 256], BF16, tag="s2")
+                for t in range(4):
+                    for a in range(2):
+                        nc.tensor.transpose(wgp[:, t, a * P:(a + 1) * P], wdup[:, a, 4 * lg + t, :], ident_b[:])
+                wgp_of[lg] = wgp
 
-        def wg_regroup(lg, wgp):
-            nc.vector.tensor_copy(out=wgg[:, lg, :, :].rearrange("p (a i b) t -> p a i b t", a=8, i=16, b=2),
-                                  in_=wgp[:].rearrange("p t (i a b) -> p a i b t", a=8, i=16, b=2))
+        def wg_regroup(pair):
+            for lg in (2 * pair, 2 * pair + 1):
+                nc.vector.tensor_copy(
+                    out=wgg[:, lg, :, :].rearrange("p (a i b) t -> p a i b t", a=8, i=16, b=2),
+                    in_=wgp_of[lg][:].rearrange("p t (i a b) -> p a i b t", a=8, i=16, b=2))
 
-        def wg_finish():
-            nc.vector.quantize_mx(out=wgw[:].rearrange("p a c -> p (a c)").bitcast(FP8X4),
-                                  scales=wgs[:].rearrange("p a c -> p (a c)"),
-                                  in_=wgg[:].rearrange("p a c t -> p (a c t)"))
+        def wg_finish(pair):
+            two = slice(2 * pair, 2 * pair + 2)
+            nc.vector.quantize_mx(out=wgw[:, two, :].rearrange("p a c -> p (a c)").bitcast(FP8X4),
+                                  scales=wgs[:, two, :].rearrange("p a c -> p (a c)"),
+                                  in_=wgg[:, two, :, :].rearrange("p a c t -> p (a c t)"))
             for d in range(4):
-                nc.vector.tensor_copy(out=wbd[32 * d:32 * d + 32, :, 256 * d:256 * d + 256].bitcast(I32),
-                                      in_=wgw[32 * d:32 * d + 32, :, :].bitcast(I32))
-                nc.vector.tensor_copy(out=wbds[32 * d:32 * d + 4, :, 256 * d:256 * d + 256].bitcast(I32),
-                                      in_=wgs[32 * d:32 * d + 4, :, :].bitcast(I32))
+                nc.vector.tensor_copy(out=wbd[32 * d:32 * d + 32, two, 256 * d:256 * d + 256].bitcast(I32),
+                                      in_=wgw[32 * d:32 * d + 32, two, :].bitcast(I32))
+                nc.vector.tensor_copy(out=wbds[32 * d:32 * d + 4, two, 256 * d:256 * d + 256].bitcast(I32),
+                                      in_=wgs[32 * d:32 * d + 4, two, :].bitcast(I32))
 
         def transposes(k):
             xs32 = xs_of[k][:].bitcast(F32)
@@ -128,7 +138,7 @@ def tile_dynamixerblock_pa_t_kernel(tc, x_seq, Wc, bc, Wg, bg, out):
             for t in range(4):
                 bank = ps_t.tile([P, 4, P], F32, tag="xt")
                 for c in range(4):
-                    nc.tensor.transpose(bank[:, c, :], xs32[:, t, c * P:(c + 1) * P], ident_f[:])
+                    nc.tensor.transpose(bank[:, c, :], xs32[:, t, c * P:(c + 1) * P], perm_f[:])
                 banks.append(bank)
             bank_of[k] = banks
 
@@ -136,11 +146,8 @@ def tile_dynamixerblock_pa_t_kernel(tc, x_seq, Wc, bc, Wg, bg, out):
             xg = xgp.tile([P, 4096], BF16, tag="xg", align_bytes=64)
             xg32 = xg[:].bitcast(F32).rearrange("p (g t n u) -> p g t n u", g=2, t=4, n=P, u=2)
             for t in range(4):
-                src = bank_of[k][t][:].rearrange("p (g u) n -> p g n u", g=2)
-                if t < 3:
-                    nc.scalar.copy(out=xg32[:, :, t, :, :], in_=src)
-                else:
-                    nc.vector.tensor_copy(out=xg32[:, :, t, :, :], in_=src)
+                nc.scalar.copy(out=xg32[:, :, t, :, :],
+                               in_=bank_of[k][t][:].rearrange("p (g u) n -> p g n u", g=2))
             return xg
 
         def quantise_x(k, xg):
@@ -165,35 +172,35 @@ def tile_dynamixerblock_pa_t_kernel(tc, x_seq, Wc, bc, Wg, bg, out):
             acc1_of[k] = accs
 
         def bias_round(k):
-            vg = vgp.tile([P, 2, P, 4], BF16, tag="vg", align_bytes=64)
+            vg = vgp.tile([P, 2, 2, 64, 4], BF16, tag="vg", align_bytes=64)
             for hh in range(2):
-                nc.scalar.activation(out=vg[:, hh, :, :],
-                                     in_=acc1_of[k][hh][:].rearrange("p (t n) -> p n t", t=4),
+                nc.scalar.activation(out=vg[:, :, hh, :, :],
+                                     in_=acc1_of[k][hh][:].rearrange("p (t a n) -> p a n t", t=4, a=2),
                                      func=ACTF.Identity, bias=bct[:, hh:hh + 1], scale=1.0)
             return vg
 
         def quantise_v(k, vg):
-            nt, lg = divmod(k, 4)
-            if lg == 0:
-                vw = vwp.tile([P, 4, 256], U32, tag="vw", align_bytes=64)
-                vsc = vwp.tile([P, 4, 256], U8, tag="vsc", align_bytes=64)
-                vw_of[nt] = (vw, vsc)
-            vw, vsc = vw_of[nt]
-            nc.vector.quantize_mx(out=vw[:, lg, :].bitcast(FP8X4), scales=vsc[:, lg, :],
-                                  in_=vg[:].rearrange("p h n t -> p (h n t)"))
+            ng, bq = divmod(k, 2)
+            if bq == 0:
+                vw = vwp.tile([P, 2, 256], U32, tag="vw", align_bytes=64)
+                vsc = vwp.tile([P, 2, 256], U8, tag="vsc", align_bytes=64)
+                vw_of[ng] = (vw, vsc)
+            vw, vsc = vw_of[ng]
+            nc.vector.quantize_mx(out=vw[:, bq, :].bitcast(FP8X4), scales=vsc[:, bq, :],
+                                  in_=vg[:].rearrange("p a h n t -> p (a h n t)"))
 
         def stage2(b):
-            nt, r = divmod(b, 4)
-            hh, half = divmod(r, 2)
-            vw, vsc = vw_of[nt]
+            ng, half = divmod(b, 2)
+            vw, vsc = vw_of[ng]
             acc2 = ps_2.tile([P, 512], F32, tag="s2")
-            for lg in range(4):
+            for i in range(4):
+                bq, a = divmod(i, 2)
                 nc.tensor.matmul_mx(out=acc2[:],
-                                    lhsT=vw[:, lg, hh * P:(hh + 1) * P].bitcast(FP8X4),
-                                    lhsT_scale=vsc[:, lg, hh * P:(hh + 1) * P],
-                                    rhs=wbd[:, lg, half * 512:(half + 1) * 512].bitcast(FP8X4),
-                                    rhs_scale=wbds[:, lg, half * 512:(half + 1) * 512],
-                                    start=(lg == 0), stop=(lg == 3))
+                                    lhsT=vw[:, bq, a * P:(a + 1) * P].bitcast(FP8X4),
+                                    lhsT_scale=vsc[:, bq, a * P:(a + 1) * P],
+                                    rhs=wbd[:, 2 * a + bq, half * 512:(half + 1) * 512].bitcast(FP8X4),
+                                    rhs_scale=wbds[:, 2 * a + bq, half * 512:(half + 1) * 512],
+                                    start=(i == 0), stop=(i == 3))
             acc2_of[b] = acc2
 
         def by_aib(ap):
@@ -202,18 +209,18 @@ def tile_dynamixerblock_pa_t_kernel(tc, x_seq, Wc, bc, Wg, bg, out):
         def by_abi(ap):
             return ap.rearrange("p (a i b) -> p a b i", a=16, i=16, b=2)
 
-        def soft_bias_max(b):
-            tt = smp.tile([P, 512], F32, tag="tt", bufs=2)
+        def soft_bias(b):
+            tt = smp.tile([P, 512], F32, tag="tt", bufs=3)
             nc.vector.tensor_tensor(out=tt[:].rearrange("p (h c) -> p h c", h=2),
                                     in0=acc2_of[b][:].rearrange("p (h c) -> p h c", h=2),
                                     in1=bgb[:].unsqueeze(1).to_broadcast([P, 2, 256]), op=ALU.add)
+            sm_of[b] = [tt]
+
+        def soft_max_sub(b):
+            tt = sm_of[b][0]
             mx = smp.tile([P, 16, 2], F32, tag="mx", bufs=2)
             nc.vector.tensor_reduce(out=mx[:], in_=by_abi(tt[:]), axis=AX.X, op=ALU.max)
-            sm_of[b] = [tt, mx]
-
-        def soft_sub(b):
-            tt, mx = sm_of[b]
-            dd = smp.tile([P, 512], F32, tag="dd", bufs=4)
+            dd = smp.tile([P, 512], F32, tag="dd", bufs=3)
             nc.gpsimd.tensor_tensor(out=by_aib(dd[:]), in0=by_aib(tt[:]),
                                     in1=mx[:].unsqueeze(2).to_broadcast([P, 16, 16, 2]), op=ALU.subtract)
             sm_of[b] = [dd]
@@ -222,62 +229,59 @@ def tile_dynamixerblock_pa_t_kernel(tc, x_seq, Wc, bc, Wg, bg, out):
             dd = sm_of[b][0]
             nc.scalar.activation(out=dd[:], in_=dd[:], func=ACTF.Exp)
 
-        def soft_sum(b):
+        def soft_norm_store(b):
             dd = sm_of[b][0]
             sm = smp.tile([P, 16, 2], F32, tag="sm", bufs=2)
             nc.vector.tensor_reduce(out=sm[:], in_=by_abi(dd[:]), axis=AX.X, op=ALU.add)
-            sm_of[b] = [dd, sm]
-
-        def soft_recip(b):
-            dd, sm = sm_of[b]
-            rs = smp.tile([P, 2, 16], F32, tag="rs", bufs=3)
+            rs = smp.tile([P, 2, 16], F32, tag="rs", bufs=2)
             nc.vector.reciprocal(out=rs[:].rearrange("p h j -> p (h j)"), in_=sm[:].rearrange("p a b -> p (a b)"))
-            sm_of[b] = [dd, rs]
-
-        def soft_norm_store(b):
-            dd, rs = sm_of[b]
             oo = smp.tile([P, 2, 16, 16], F32, tag="oo", bufs=3)
             for h in range(2):
-                nc.gpsimd.tensor_tensor(
+                nc.vector.tensor_tensor(
                     out=oo[:, h, :, :].rearrange("p i (a b) -> p i a b", b=2),
                     in0=dd[:, h * 256:(h + 1) * 256].rearrange("p (a i b) -> p i a b", a=8, i=16, b=2),
                     in1=rs[:, h, :].rearrange("p (a b) -> p a b", b=2).unsqueeze(1).to_broadcast([P, 16, 8, 2]),
                     op=ALU.mult)
-            nt, r = divmod(b, 4)
-            nc.sync.dma_start(out=out_rows[nt][:, r * 512:(r + 1) * 512],
-                              in_=oo[:].rearrange("p h i j -> p (h i j)"))
+            ng, half = divmod(b, 2)
+            for hh in range(2):
+                nc.sync.dma_start(out=out_rows[ng, hh][:, half * 512:(half + 1) * 512],
+                                  in_=oo[hh * 64:(hh + 1) * 64].rearrange("p h i j -> p (h i j)"))
 
         def has(i, n):
             return 0 <= i < n
 
-        for q in range(-1, N_BANKS + 8):
+        for q in range(-1, N_BANKS + 5):
             if has(q + PREFETCH, N_UNITS) and q >= 0:
                 load(q + PREFETCH)
+            if q == 1:
+                wg_transposes(1)
             if has(q + 1, N_UNITS):
                 transposes(q + 1)
-            wgp = wg_transposes(q) if has(q, 4) else None
-            if has(q - 7, N_BANKS):
-                soft_norm_store(q - 7)
+            if q == -1:
+                wg_transposes(0)
+            if has(q - 4, N_BANKS):
+                soft_max_sub(q - 4)
+            if has(q - 3, N_BANKS):
+                soft_bias(q - 3)
             if has(q - 5, N_BANKS):
-                soft_bias_max(q - 5)
-                soft_sub(q - 5)
+                soft_norm_store(q - 5)
+            if q == 1:
+                wg_regroup(1)
+            if q == 2:
+                wg_finish(1)
             xg = regroup(q + 1) if has(q + 1, N_UNITS) else None
-            if has(q - 6, N_BANKS):
-                soft_sum(q - 6)
             if has(q, N_UNITS):
                 stage1(q)
-            if has(q - 4, N_BANKS):
-                stage2(q - 4)
+            if has(q - 2, N_BANKS):
+                stage2(q - 2)
             vg = bias_round(q) if has(q, N_UNITS) else None
-            if wgp is not None:
-                wg_regroup(q, wgp)
             if xg is not None:
                 quantise_x(q + 1, xg)
-            if has(q - 5, N_BANKS):
-                soft_exp(q - 5)
+            if q == -1:
+                wg_regroup(0)
+            if has(q - 4, N_BANKS):
+                soft_exp(q - 4)
             if vg is not None:
                 quantise_v(q, vg)
-            if has(q - 6, N_BANKS):
-                soft_recip(q - 6)
-            if q == 3:
-                wg_finish()
+            if q == 0:
+                wg_finish(0)

@@ -46,6 +46,7 @@ def tile_dynamixerblock_pa_t_kernel(tc, x_seq, Wc, bc, Wg, bg, out):
         acc2_of = {}
         sm_of = {}
         wgp_of = {}
+        xg_of = {}
 
         wc_sb = const.tile([P, 2, 1024], BF16, tag="wc_sb")
         nc.sync.dma_start(out=wc_sb[:], in_=Wc.rearrange("(h p) k -> p h k", p=P))
@@ -72,7 +73,7 @@ def tile_dynamixerblock_pa_t_kernel(tc, x_seq, Wc, bc, Wg, bg, out):
         make_identity(nc, ident_b[:])
 
         wbd = const.tile([P, 4, 1024], U32, tag="wbd", align_bytes=64)
-        wbds = const.tile([P, 4, 1024], U8, tag="wbds", align_bytes=64)
+        wbds = const.tile([P, 4, 512], U8, tag="wbds", align_bytes=64)
         nc.vector.memset(wbd[:].bitcast(I32), 0)
         nc.vector.memset(wbds[:].bitcast(I32), 0)
         perm_f = const.tile([P, P], F32, tag="perm_f")
@@ -99,13 +100,15 @@ def tile_dynamixerblock_pa_t_kernel(tc, x_seq, Wc, bc, Wg, bg, out):
         nc.vector.quantize_mx(out=wcw[:].bitcast(FP8X4), scales=wcs[:], in_=wcg[:])
 
         wdup = const.tile([P, 2, 16, P], BF16, tag="wdup")
+        nc.vector.tensor_copy(
+            out=wdup[:, 0, :, :].rearrange("p l (d r) -> p l d r", d=4),
+            in_=wg_sb[:, 0, :].rearrange("p (l r) -> p l r", r=32).unsqueeze(2).to_broadcast([P, 16, 4, 32]))
         nc.gpsimd.tensor_scalar(
-            out=wdup[:].rearrange("p a l (d r) -> p (a l) d r", d=4),
-            in0=wg_sb[:].rearrange("p a (l r) -> p (a l) r", r=32).unsqueeze(2).to_broadcast([P, 32, 4, 32]),
+            out=wdup[:, 1, :, :].rearrange("p l (d r) -> p l d r", d=4),
+            in0=wg_sb[:, 1, :].rearrange("p (l r) -> p l r", r=32).unsqueeze(2).to_broadcast([P, 16, 4, 32]),
             scalar1=1.0, scalar2=0.0, op0=ALU.mult, op1=ALU.add)
         wgg = const.tile([P, 4, 256, 4], BF16, tag="wgg", align_bytes=64)
         wgw = const.tile([P, 4, 256], U32, tag="wgw", align_bytes=64)
-        wgs = const.tile([P, 4, 256], U8, tag="wgs", align_bytes=64)
 
         def wg_transposes(pair):
             for lg in (2 * pair, 2 * pair + 1):
@@ -117,40 +120,39 @@ def tile_dynamixerblock_pa_t_kernel(tc, x_seq, Wc, bc, Wg, bg, out):
 
         def wg_regroup(pair):
             for lg in (2 * pair, 2 * pair + 1):
-                nc.vector.tensor_copy(
-                    out=wgg[:, lg, :, :].rearrange("p (a i b) t -> p a i b t", a=8, i=16, b=2),
-                    in_=wgp_of[lg][:].rearrange("p t (i a b) -> p a i b t", a=8, i=16, b=2))
+                dst = wgg[:, lg, :, :].rearrange("p (a i b) t -> p a i b t", a=8, i=16, b=2)
+                src = wgp_of[lg][:].rearrange("p t (i a b) -> p a i b t", a=8, i=16, b=2)
+                nc.vector.tensor_copy(out=dst, in_=src)
 
         def wg_finish(pair):
             two = slice(2 * pair, 2 * pair + 2)
-            nc.vector.quantize_mx(out=wgw[:, two, :].rearrange("p a c -> p (a c)").bitcast(FP8X4),
-                                  scales=wgs[:, two, :].rearrange("p a c -> p (a c)"),
-                                  in_=wgg[:, two, :, :].rearrange("p a c t -> p (a c t)"))
+            for lg in (2 * pair, 2 * pair + 1):
+                nc.vector.quantize_mx(out=wgw[:, lg, :].bitcast(FP8X4), scales=wbds[:, lg, 0:256],
+                                      in_=wgg[:, lg, :, :].rearrange("p c t -> p (c t)"))
             for d in range(4):
                 nc.vector.tensor_copy(out=wbd[32 * d:32 * d + 32, two, 256 * d:256 * d + 256].bitcast(I32),
                                       in_=wgw[32 * d:32 * d + 32, two, :].bitcast(I32))
-                nc.vector.tensor_copy(out=wbds[32 * d:32 * d + 4, two, 256 * d:256 * d + 256].bitcast(I32),
-                                      in_=wgs[32 * d:32 * d + 4, two, :].bitcast(I32))
+            nc.vector.tensor_copy(out=wbds[:, two, 256:512].bitcast(I32), in_=wbds[:, two, 0:256].bitcast(I32))
 
-        def transposes(k):
+        def transposes(k, part):
             xs32 = xs_of[k][:].bitcast(F32)
-            banks = []
-            for t in range(4):
+            for t in (2 * part, 2 * part + 1):
                 bank = ps_t.tile([P, 4, P], F32, tag="xt")
                 for c in range(4):
                     nc.tensor.transpose(bank[:, c, :], xs32[:, t, c * P:(c + 1) * P], perm_f[:])
-                banks.append(bank)
-            bank_of[k] = banks
+                bank_of[(k, t)] = bank
 
-        def regroup(k):
-            xg = xgp.tile([P, 4096], BF16, tag="xg", align_bytes=64)
-            xg32 = xg[:].bitcast(F32).rearrange("p (g t n u) -> p g t n u", g=2, t=4, n=P, u=2)
-            for t in range(4):
+        def regroup(k, part):
+            if part == 0:
+                xg_new = xgp.tile([P, 4096], BF16, tag="xg", align_bytes=64)
+                xg_of[k] = xg_new
+            xg32 = xg_of[k][:].bitcast(F32).rearrange("p (g t n u) -> p g t n u", g=2, t=4, n=P, u=2)
+            for t in (2 * part, 2 * part + 1):
                 nc.scalar.copy(out=xg32[:, :, t, :, :],
-                               in_=bank_of[k][t][:].rearrange("p (g u) n -> p g n u", g=2))
-            return xg
+                               in_=bank_of[(k, t)][:].rearrange("p (g u) n -> p g n u", g=2))
 
-        def quantise_x(k, xg):
+        def quantise_x(k):
+            xg = xg_of[k]
             xw = xwp.tile([P, 1024], U32, tag="xw", align_bytes=64)
             xsc = xwp.tile([P, 1024], U8, tag="xsc", align_bytes=64)
             nc.vector.quantize_mx(out=xw[:].bitcast(FP8X4), scales=xsc[:], in_=xg[:])
@@ -199,7 +201,7 @@ def tile_dynamixerblock_pa_t_kernel(tc, x_seq, Wc, bc, Wg, bg, out):
                                     lhsT=vw[:, bq, a * P:(a + 1) * P].bitcast(FP8X4),
                                     lhsT_scale=vsc[:, bq, a * P:(a + 1) * P],
                                     rhs=wbd[:, 2 * a + bq, half * 512:(half + 1) * 512].bitcast(FP8X4),
-                                    rhs_scale=wbds[:, 2 * a + bq, half * 512:(half + 1) * 512],
+                                    rhs_scale=wbds[:, 2 * a + bq, :],
                                     start=(i == 0), stop=(i == 3))
             acc2_of[b] = acc2
 
@@ -250,38 +252,38 @@ def tile_dynamixerblock_pa_t_kernel(tc, x_seq, Wc, bc, Wg, bg, out):
         def has(i, n):
             return 0 <= i < n
 
-        for q in range(-1, N_BANKS + 5):
+        for q in range(-1, N_BANKS + 7):
             if has(q + PREFETCH, N_UNITS) and q >= 0:
                 load(q + PREFETCH)
-            if q == 1:
-                wg_transposes(1)
+            if has(q, N_UNITS):
+                quantise_x(q)
+            if has(q - 1, N_UNITS):
+                quantise_v(q - 1, bias_round(q - 1))
             if has(q + 1, N_UNITS):
-                transposes(q + 1)
+                transposes(q + 1, 0)
             if q == -1:
                 wg_transposes(0)
-            if has(q - 4, N_BANKS):
-                soft_max_sub(q - 4)
             if has(q - 3, N_BANKS):
-                soft_bias(q - 3)
+                stage2(q - 3)
+            if has(q + 1, N_UNITS):
+                regroup(q + 1, 0)
+            if q == -1 or q == 1:
+                wg_regroup((q + 1) // 2)
+            if q == 0 or q == 2:
+                wg_finish(q // 2)
             if has(q - 5, N_BANKS):
-                soft_norm_store(q - 5)
-            if q == 1:
-                wg_regroup(1)
-            if q == 2:
-                wg_finish(1)
-            xg = regroup(q + 1) if has(q + 1, N_UNITS) else None
+                soft_max_sub(q - 5)
+            if has(q - 4, N_BANKS):
+                soft_bias(q - 4)
+            if has(q - 6, N_BANKS):
+                soft_norm_store(q - 6)
+            if has(q + 1, N_UNITS):
+                transposes(q + 1, 1)
+            if q == 0:
+                wg_transposes(1)
             if has(q, N_UNITS):
                 stage1(q)
-            if has(q - 2, N_BANKS):
-                stage2(q - 2)
-            vg = bias_round(q) if has(q, N_UNITS) else None
-            if xg is not None:
-                quantise_x(q + 1, xg)
-            if q == -1:
-                wg_regroup(0)
-            if has(q - 4, N_BANKS):
-                soft_exp(q - 4)
-            if vg is not None:
-                quantise_v(q, vg)
-            if q == 0:
-                wg_finish(0)
+            if has(q + 1, N_UNITS):
+                regroup(q + 1, 1)
+            if has(q - 5, N_BANKS):
+                soft_exp(q - 5)

@@ -83,8 +83,8 @@ def tile_dynamixerblock_pa_t_kernel(tc, x_seq, Wc, bc, Wg, bg, out):
         bct = const.tile([P, 2], F32, tag="bct")
         nc.vector.tensor_copy(out=bct[:], in_=bc_b[:])
         bgb = const.tile([P, 256], F32, tag="bgb")
-        nc.vector.tensor_copy(out=bgb[:].rearrange("p (a i b) -> p a i b", a=8, i=16, b=2),
-                              in_=bg_b[:].rearrange("p (i a b) -> p a i b", a=8, i=16, b=2))
+        nc.vector.tensor_copy(out=bgb[:].rearrange("p (j i) -> p j i", i=16),
+                              in_=bg_b[:].rearrange("p (i j) -> p j i", i=16))
 
         wcg = const.tile([P, 2048], BF16, tag="wcg", align_bytes=64)
         wcg32 = wcg[:].bitcast(F32).rearrange("p (g h m u) -> p g h m u", g=2, h=2, m=P, u=2)
@@ -120,9 +120,8 @@ def tile_dynamixerblock_pa_t_kernel(tc, x_seq, Wc, bc, Wg, bg, out):
 
         def wg_regroup(pair):
             for lg in (2 * pair, 2 * pair + 1):
-                dst = wgg[:, lg, :, :].rearrange("p (a i b) t -> p a i b t", a=8, i=16, b=2)
-                src = wgp_of[lg][:].rearrange("p t (i a b) -> p a i b t", a=8, i=16, b=2)
-                nc.vector.tensor_copy(out=dst, in_=src)
+                nc.vector.tensor_copy(out=wgg[:, lg, :, :].rearrange("p (j i) t -> p j i t", i=16),
+                                      in_=wgp_of[lg][:].rearrange("p t (i j) -> p j i t", i=16))
 
         def wg_finish(pair):
             two = slice(2 * pair, 2 * pair + 2)
@@ -134,25 +133,25 @@ def tile_dynamixerblock_pa_t_kernel(tc, x_seq, Wc, bc, Wg, bg, out):
                                       in_=wgw[32 * d:32 * d + 32, two, :].bitcast(I32))
             nc.vector.tensor_copy(out=wbds[:, two, 256:512].bitcast(I32), in_=wbds[:, two, 0:256].bitcast(I32))
 
-        def transposes(k, part):
+        def transposes(k):
             xs32 = xs_of[k][:].bitcast(F32)
-            for t in (2 * part, 2 * part + 1):
+            banks = []
+            for t in range(4):
                 bank = ps_t.tile([P, 4, P], F32, tag="xt")
                 for c in range(4):
                     nc.tensor.transpose(bank[:, c, :], xs32[:, t, c * P:(c + 1) * P], perm_f[:])
-                bank_of[(k, t)] = bank
+                banks.append(bank)
+            bank_of[k] = banks
 
-        def regroup(k, part):
-            if part == 0:
-                xg_new = xgp.tile([P, 4096], BF16, tag="xg", align_bytes=64)
-                xg_of[k] = xg_new
-            xg32 = xg_of[k][:].bitcast(F32).rearrange("p (g t n u) -> p g t n u", g=2, t=4, n=P, u=2)
-            for t in (2 * part, 2 * part + 1):
+        def regroup(k):
+            xg = xgp.tile([P, 4096], BF16, tag="xg", align_bytes=64)
+            xg32 = xg[:].bitcast(F32).rearrange("p (g t n u) -> p g t n u", g=2, t=4, n=P, u=2)
+            for t in range(4):
                 nc.scalar.copy(out=xg32[:, :, t, :, :],
-                               in_=bank_of[(k, t)][:].rearrange("p (g u) n -> p g n u", g=2))
+                               in_=bank_of[k][t][:].rearrange("p (g u) n -> p g n u", g=2))
+            return xg
 
-        def quantise_x(k):
-            xg = xg_of[k]
+        def quantise_x(k, xg):
             xw = xwp.tile([P, 1024], U32, tag="xw", align_bytes=64)
             xsc = xwp.tile([P, 1024], U8, tag="xsc", align_bytes=64)
             nc.vector.quantize_mx(out=xw[:].bitcast(FP8X4), scales=xsc[:], in_=xg[:])
@@ -205,11 +204,11 @@ def tile_dynamixerblock_pa_t_kernel(tc, x_seq, Wc, bc, Wg, bg, out):
                                     start=(i == 0), stop=(i == 3))
             acc2_of[b] = acc2
 
-        def by_aib(ap):
-            return ap.rearrange("p (a i b) -> p a i b", a=16, i=16, b=2)
+        def rows(ap):
+            return ap.rearrange("p (r i) -> p r i", i=16)
 
-        def by_abi(ap):
-            return ap.rearrange("p (a i b) -> p a b i", a=16, i=16, b=2)
+        def helper(b):
+            return nc.vector if b >= N_BANKS - 2 else nc.gpsimd
 
         def soft_bias(b):
             tt = smp.tile([P, 512], F32, tag="tt", bufs=3)
@@ -220,30 +219,35 @@ def tile_dynamixerblock_pa_t_kernel(tc, x_seq, Wc, bc, Wg, bg, out):
 
         def soft_max_sub(b):
             tt = sm_of[b][0]
-            mx = smp.tile([P, 16, 2], F32, tag="mx", bufs=2)
-            nc.vector.tensor_reduce(out=mx[:], in_=by_abi(tt[:]), axis=AX.X, op=ALU.max)
-            dd = smp.tile([P, 512], F32, tag="dd", bufs=3)
-            nc.gpsimd.tensor_tensor(out=by_aib(dd[:]), in0=by_aib(tt[:]),
-                                    in1=mx[:].unsqueeze(2).to_broadcast([P, 16, 16, 2]), op=ALU.subtract)
+            mx = smp.tile([P, 32], F32, tag="mx", bufs=2)
+            nc.vector.tensor_reduce(out=mx[:], in_=rows(tt[:]), axis=AX.X, op=ALU.max)
+            dd = smp.tile([P, 512], F32, tag="dd", bufs=4)
+            helper(b).tensor_tensor(out=rows(dd[:]), in0=rows(tt[:]),
+                                    in1=mx[:].unsqueeze(2).to_broadcast([P, 32, 16]), op=ALU.subtract)
             sm_of[b] = [dd]
 
         def soft_exp(b):
             dd = sm_of[b][0]
             nc.scalar.activation(out=dd[:], in_=dd[:], func=ACTF.Exp)
 
-        def soft_norm_store(b):
+        def soft_sum(b):
             dd = sm_of[b][0]
-            sm = smp.tile([P, 16, 2], F32, tag="sm", bufs=2)
-            nc.vector.tensor_reduce(out=sm[:], in_=by_abi(dd[:]), axis=AX.X, op=ALU.add)
-            rs = smp.tile([P, 2, 16], F32, tag="rs", bufs=2)
-            nc.vector.reciprocal(out=rs[:].rearrange("p h j -> p (h j)"), in_=sm[:].rearrange("p a b -> p (a b)"))
+            sm = smp.tile([P, 32], F32, tag="sm", bufs=2)
+            nc.vector.tensor_reduce(out=sm[:], in_=rows(dd[:]), axis=AX.X, op=ALU.add)
+            sm_of[b] = [dd, sm]
+
+        def soft_recip(b):
+            dd, sm = sm_of[b]
+            rs = smp.tile([P, 2, 16], F32, tag="rs", bufs=3)
+            nc.vector.reciprocal(out=rs[:].rearrange("p h j -> p (h j)"), in_=sm[:])
+            sm_of[b] = [dd, rs]
+
+        def soft_norm_store(b):
+            dd, rs = sm_of[b]
             oo = smp.tile([P, 2, 16, 16], F32, tag="oo", bufs=3)
-            for h in range(2):
-                nc.vector.tensor_tensor(
-                    out=oo[:, h, :, :].rearrange("p i (a b) -> p i a b", b=2),
-                    in0=dd[:, h * 256:(h + 1) * 256].rearrange("p (a i b) -> p i a b", a=8, i=16, b=2),
-                    in1=rs[:, h, :].rearrange("p (a b) -> p a b", b=2).unsqueeze(1).to_broadcast([P, 16, 8, 2]),
-                    op=ALU.mult)
+            helper(b).tensor_tensor(out=oo[:],
+                                    in0=dd[:].rearrange("p (h j i) -> p h i j", h=2, i=16),
+                                    in1=rs[:].unsqueeze(2).to_broadcast([P, 2, 16, 16]), op=ALU.mult)
             ng, half = divmod(b, 2)
             for hh in range(2):
                 nc.sync.dma_start(out=out_rows[ng, hh][:, half * 512:(half + 1) * 512],
@@ -255,35 +259,37 @@ def tile_dynamixerblock_pa_t_kernel(tc, x_seq, Wc, bc, Wg, bg, out):
         for q in range(-1, N_BANKS + 7):
             if has(q + PREFETCH, N_UNITS) and q >= 0:
                 load(q + PREFETCH)
-            if has(q, N_UNITS):
-                quantise_x(q)
-            if has(q - 1, N_UNITS):
-                quantise_v(q - 1, bias_round(q - 1))
             if has(q + 1, N_UNITS):
-                transposes(q + 1, 0)
+                transposes(q + 1)
             if q == -1:
                 wg_transposes(0)
-            if has(q - 3, N_BANKS):
-                stage2(q - 3)
-            if has(q + 1, N_UNITS):
-                regroup(q + 1, 0)
-            if q == -1 or q == 1:
-                wg_regroup((q + 1) // 2)
-            if q == 0 or q == 2:
-                wg_finish(q // 2)
-            if has(q - 5, N_BANKS):
-                soft_max_sub(q - 5)
-            if has(q - 4, N_BANKS):
-                soft_bias(q - 4)
             if has(q - 6, N_BANKS):
                 soft_norm_store(q - 6)
-            if has(q + 1, N_UNITS):
-                transposes(q + 1, 1)
-            if q == 0:
-                wg_transposes(1)
+            if has(q - 4, N_BANKS):
+                soft_max_sub(q - 4)
+            if has(q - 3, N_BANKS):
+                soft_bias(q - 3)
+            if has(q - 5, N_BANKS):
+                soft_sum(q - 5)
+            if q == 1:
+                wg_regroup(1)
+            xg = regroup(q + 1) if has(q + 1, N_UNITS) else None
             if has(q, N_UNITS):
                 stage1(q)
-            if has(q + 1, N_UNITS):
-                regroup(q + 1, 1)
+            if has(q - 2, N_BANKS):
+                stage2(q - 2)
+            if q == 0:
+                wg_transposes(1)
+            vg = bias_round(q) if has(q, N_UNITS) else None
+            if xg is not None:
+                quantise_x(q + 1, xg)
+            if q == -1:
+                wg_regroup(0)
+            if has(q - 4, N_BANKS):
+                soft_exp(q - 4)
+            if vg is not None:
+                quantise_v(q, vg)
             if has(q - 5, N_BANKS):
-                soft_exp(q - 5)
+                soft_recip(q - 5)
+            if q == 0 or q == 1:
+                wg_finish(q)

@@ -46,7 +46,10 @@ def tile_dynamixerblock_pa_t_kernel(tc, x_seq, Wc, bc, Wg, bg, out):
         acc2_of = {}
         sm_of = {}
         wgp_of = {}
-        xg_of = {}
+        tt_of = {}
+        mx_of = {}
+        dd_of = {}
+        rs_of = {}
 
         wc_sb = const.tile([P, 2, 1024], BF16, tag="wc_sb")
         nc.sync.dma_start(out=wc_sb[:], in_=Wc.rearrange("(h p) k -> p h k", p=P))
@@ -83,8 +86,8 @@ def tile_dynamixerblock_pa_t_kernel(tc, x_seq, Wc, bc, Wg, bg, out):
         bct = const.tile([P, 2], F32, tag="bct")
         nc.vector.tensor_copy(out=bct[:], in_=bc_b[:])
         bgb = const.tile([P, 256], F32, tag="bgb")
-        nc.vector.tensor_copy(out=bgb[:].rearrange("p (j i) -> p j i", i=16),
-                              in_=bg_b[:].rearrange("p (i j) -> p j i", i=16))
+        nc.vector.tensor_copy(out=bgb[:].rearrange("p (a i b) -> p a i b", a=8, i=16, b=2),
+                              in_=bg_b[:].rearrange("p (i a b) -> p a i b", a=8, i=16, b=2))
 
         wcg = const.tile([P, 2048], BF16, tag="wcg", align_bytes=64)
         wcg32 = wcg[:].bitcast(F32).rearrange("p (g h m u) -> p g h m u", g=2, h=2, m=P, u=2)
@@ -120,8 +123,9 @@ def tile_dynamixerblock_pa_t_kernel(tc, x_seq, Wc, bc, Wg, bg, out):
 
         def wg_regroup(pair):
             for lg in (2 * pair, 2 * pair + 1):
-                nc.vector.tensor_copy(out=wgg[:, lg, :, :].rearrange("p (j i) t -> p j i t", i=16),
-                                      in_=wgp_of[lg][:].rearrange("p t (i j) -> p j i t", i=16))
+                dst = wgg[:, lg, :, :].rearrange("p (a i b) t -> p a i b t", a=8, i=16, b=2)
+                src = wgp_of[lg][:].rearrange("p t (i a b) -> p a i b t", a=8, i=16, b=2)
+                nc.vector.tensor_copy(out=dst, in_=src)
 
         def wg_finish(pair):
             two = slice(2 * pair, 2 * pair + 2)
@@ -204,50 +208,51 @@ def tile_dynamixerblock_pa_t_kernel(tc, x_seq, Wc, bc, Wg, bg, out):
                                     start=(i == 0), stop=(i == 3))
             acc2_of[b] = acc2
 
-        def rows(ap):
-            return ap.rearrange("p (r i) -> p r i", i=16)
+        def by_aib(ap):
+            return ap.rearrange("p (a i b) -> p a i b", a=16, i=16, b=2)
 
-        def helper(b):
-            return nc.vector if b >= N_BANKS - 2 else nc.gpsimd
+        def by_abi(ap):
+            return ap.rearrange("p (a i b) -> p a b i", a=16, i=16, b=2)
 
         def soft_bias(b):
             tt = smp.tile([P, 512], F32, tag="tt", bufs=3)
             nc.vector.tensor_tensor(out=tt[:].rearrange("p (h c) -> p h c", h=2),
                                     in0=acc2_of[b][:].rearrange("p (h c) -> p h c", h=2),
                                     in1=bgb[:].unsqueeze(1).to_broadcast([P, 2, 256]), op=ALU.add)
-            sm_of[b] = [tt]
+            tt_of[b] = tt
 
-        def soft_max_sub(b):
-            tt = sm_of[b][0]
-            mx = smp.tile([P, 32], F32, tag="mx", bufs=2)
-            nc.vector.tensor_reduce(out=mx[:], in_=rows(tt[:]), axis=AX.X, op=ALU.max)
-            dd = smp.tile([P, 512], F32, tag="dd", bufs=4)
-            helper(b).tensor_tensor(out=rows(dd[:]), in0=rows(tt[:]),
-                                    in1=mx[:].unsqueeze(2).to_broadcast([P, 32, 16]), op=ALU.subtract)
-            sm_of[b] = [dd]
+        def soft_max(b):
+            mx = smp.tile([P, 16, 2], F32, tag="mx", bufs=2)
+            nc.vector.tensor_reduce(out=mx[:], in_=by_abi(tt_of[b][:]), axis=AX.X, op=ALU.max)
+            mx_of[b] = mx
+
+        def soft_sub(b):
+            dd = smp.tile([P, 512], F32, tag="dd", bufs=3)
+            nc.vector.tensor_tensor(out=by_aib(dd[:]), in0=by_aib(tt_of[b][:]),
+                                    in1=mx_of[b][:].unsqueeze(2).to_broadcast([P, 16, 16, 2]), op=ALU.subtract)
+            dd_of[b] = dd
 
         def soft_exp(b):
-            dd = sm_of[b][0]
-            nc.scalar.activation(out=dd[:], in_=dd[:], func=ACTF.Exp)
+            nc.scalar.activation(out=dd_of[b][:], in_=dd_of[b][:], func=ACTF.Exp)
 
         def soft_sum(b):
-            dd = sm_of[b][0]
-            sm = smp.tile([P, 32], F32, tag="sm", bufs=2)
-            nc.vector.tensor_reduce(out=sm[:], in_=rows(dd[:]), axis=AX.X, op=ALU.add)
-            sm_of[b] = [dd, sm]
+            sm = smp.tile([P, 16, 2], F32, tag="sm", bufs=2)
+            nc.vector.tensor_reduce(out=sm[:], in_=by_abi(dd_of[b][:]), axis=AX.X, op=ALU.add)
+            sm_of[b] = sm
 
         def soft_recip(b):
-            dd, sm = sm_of[b]
-            rs = smp.tile([P, 2, 16], F32, tag="rs", bufs=3)
-            nc.vector.reciprocal(out=rs[:].rearrange("p h j -> p (h j)"), in_=sm[:])
-            sm_of[b] = [dd, rs]
+            rs = smp.tile([P, 2, 16], F32, tag="rs", bufs=2)
+            nc.vector.reciprocal(out=rs[:].rearrange("p h j -> p (h j)"), in_=sm_of[b][:].rearrange("p a b -> p (a b)"))
+            rs_of[b] = rs
 
         def soft_norm_store(b):
-            dd, rs = sm_of[b]
             oo = smp.tile([P, 2, 16, 16], F32, tag="oo", bufs=3)
-            helper(b).tensor_tensor(out=oo[:],
-                                    in0=dd[:].rearrange("p (h j i) -> p h i j", h=2, i=16),
-                                    in1=rs[:].unsqueeze(2).to_broadcast([P, 2, 16, 16]), op=ALU.mult)
+            for h in range(2):
+                nc.vector.tensor_tensor(
+                    out=oo[:, h, :, :].rearrange("p i (a b) -> p i a b", b=2),
+                    in0=dd_of[b][:, h * 256:(h + 1) * 256].rearrange("p (a i b) -> p i a b", a=8, i=16, b=2),
+                    in1=rs_of[b][:, h, :].rearrange("p (a b) -> p a b", b=2).unsqueeze(1).to_broadcast([P, 16, 8, 2]),
+                    op=ALU.mult)
             ng, half = divmod(b, 2)
             for hh in range(2):
                 nc.sync.dma_start(out=out_rows[ng, hh][:, half * 512:(half + 1) * 512],
@@ -256,21 +261,25 @@ def tile_dynamixerblock_pa_t_kernel(tc, x_seq, Wc, bc, Wg, bg, out):
         def has(i, n):
             return 0 <= i < n
 
-        for q in range(-1, N_BANKS + 7):
+        for q in range(-1, N_BANKS + 6):
             if has(q + PREFETCH, N_UNITS) and q >= 0:
                 load(q + PREFETCH)
             if has(q + 1, N_UNITS):
                 transposes(q + 1)
             if q == -1:
                 wg_transposes(0)
-            if has(q - 6, N_BANKS):
-                soft_norm_store(q - 6)
-            if has(q - 4, N_BANKS):
-                soft_max_sub(q - 4)
-            if has(q - 3, N_BANKS):
-                soft_bias(q - 3)
             if has(q - 5, N_BANKS):
                 soft_sum(q - 5)
+            if has(q - 4, N_BANKS):
+                soft_max(q - 4)
+            if has(q - 5, N_BANKS):
+                soft_recip(q - 5)
+            if has(q - 3, N_BANKS):
+                soft_bias(q - 3)
+            if has(q - 4, N_BANKS):
+                soft_sub(q - 4)
+            if has(q - 5, N_BANKS):
+                soft_norm_store(q - 5)
             if q == 1:
                 wg_regroup(1)
             xg = regroup(q + 1) if has(q + 1, N_UNITS) else None
@@ -289,7 +298,5 @@ def tile_dynamixerblock_pa_t_kernel(tc, x_seq, Wc, bc, Wg, bg, out):
                 soft_exp(q - 4)
             if vg is not None:
                 quantise_v(q, vg)
-            if has(q - 5, N_BANKS):
-                soft_recip(q - 5)
             if q == 0 or q == 1:
                 wg_finish(q)

@@ -47,6 +47,7 @@ def tile_dynamixerblock_pa_t_kernel(tc, x_seq, Wc, bc, Wg, bg, out):
         sm_of = {}
         wgp_of = {}
         tt_of = {}
+        vg_of = {}
         mx_of = {}
         dd_of = {}
         rs_of = {}
@@ -64,7 +65,12 @@ def tile_dynamixerblock_pa_t_kernel(tc, x_seq, Wc, bc, Wg, bg, out):
         def load(k):
             ng, bq = divmod(k, 2)
             xs = xin.tile([P, 4, 1024], BF16, tag="xs")
-            nc.sync.dma_start(out=xs[:], in_=x_rows[ng * P:(ng + 1) * P, 4 * bq:4 * bq + 4, :])
+            src = x_rows[ng * P:(ng + 1) * P, 4 * bq:4 * bq + 4, :]
+            if k == 0:
+                for t in range(4):
+                    nc.sync.dma_start(out=xs[:, t, :], in_=src[:, t, :])
+            else:
+                nc.sync.dma_start(out=xs[:], in_=src)
             xs_of[k] = xs
 
         for k in range(PREFETCH):
@@ -151,8 +157,8 @@ def tile_dynamixerblock_pa_t_kernel(tc, x_seq, Wc, bc, Wg, bg, out):
             xg = xgp.tile([P, 4096], BF16, tag="xg", align_bytes=64)
             xg32 = xg[:].bitcast(F32).rearrange("p (g t n u) -> p g t n u", g=2, t=4, n=P, u=2)
             for t in range(4):
-                nc.scalar.copy(out=xg32[:, :, t, :, :],
-                               in_=bank_of[k][t][:].rearrange("p (g u) n -> p g n u", g=2))
+                copy = nc.vector.tensor_copy if (k == 0 and t % 2 == 1) else nc.scalar.copy
+                copy(out=xg32[:, :, t, :, :], in_=bank_of[k][t][:].rearrange("p (g u) n -> p g n u", g=2))
             return xg
 
         def quantise_x(k, xg):
@@ -177,22 +183,22 @@ def tile_dynamixerblock_pa_t_kernel(tc, x_seq, Wc, bc, Wg, bg, out):
             acc1_of[k] = accs
 
         def bias_round(k):
-            vg = vgp.tile([P, 2, 2, 64, 4], BF16, tag="vg", align_bytes=64)
-            for hh in range(2):
-                nc.scalar.activation(out=vg[:, :, hh, :, :],
-                                     in_=acc1_of[k][hh][:].rearrange("p (t a n) -> p a n t", t=4, a=2),
-                                     func=ACTF.Identity, bias=bct[:, hh:hh + 1], scale=1.0)
-            return vg
-
-        def quantise_v(k, vg):
             ng, bq = divmod(k, 2)
             if bq == 0:
-                vw = vwp.tile([P, 2, 256], U32, tag="vw", align_bytes=64)
-                vsc = vwp.tile([P, 2, 256], U8, tag="vsc", align_bytes=64)
-                vw_of[ng] = (vw, vsc)
-            vw, vsc = vw_of[ng]
-            nc.vector.quantize_mx(out=vw[:, bq, :].bitcast(FP8X4), scales=vsc[:, bq, :],
-                                  in_=vg[:].rearrange("p a h n t -> p (a h n t)"))
+                vg_new = vgp.tile([P, 2, 2, 2, 64, 4], BF16, tag="vg", align_bytes=64)
+                vg_of[ng] = vg_new
+            for hh in range(2):
+                nc.scalar.activation(out=vg_of[ng][:, bq, :, hh, :, :],
+                                     in_=acc1_of[k][hh][:].rearrange("p (t a n) -> p a n t", t=4, a=2),
+                                     func=ACTF.Identity, bias=bct[:, hh:hh + 1], scale=1.0)
+
+        def quantise_v(ng):
+            vw = vwp.tile([P, 2, 256], U32, tag="vw", align_bytes=64)
+            vsc = vwp.tile([P, 2, 256], U8, tag="vsc", align_bytes=64)
+            nc.vector.quantize_mx(out=vw[:].rearrange("p q c -> p (q c)").bitcast(FP8X4),
+                                  scales=vsc[:].rearrange("p q c -> p (q c)"),
+                                  in_=vg_of[ng][:].rearrange("p q a h n t -> p (q a h n t)"))
+            vw_of[ng] = (vw, vsc)
 
         def stage2(b):
             ng, half = divmod(b, 2)
@@ -227,8 +233,9 @@ def tile_dynamixerblock_pa_t_kernel(tc, x_seq, Wc, bc, Wg, bg, out):
             mx_of[b] = mx
 
         def soft_sub(b):
-            dd = smp.tile([P, 512], F32, tag="dd", bufs=3)
-            nc.vector.tensor_tensor(out=by_aib(dd[:]), in0=by_aib(tt_of[b][:]),
+            dd = smp.tile([P, 512], F32, tag="dd", bufs=4)
+            eng = nc.vector if b >= N_BANKS - 2 else nc.gpsimd
+            eng.tensor_tensor(out=by_aib(dd[:]), in0=by_aib(tt_of[b][:]),
                                     in1=mx_of[b][:].unsqueeze(2).to_broadcast([P, 16, 16, 2]), op=ALU.subtract)
             dd_of[b] = dd
 
@@ -241,7 +248,7 @@ def tile_dynamixerblock_pa_t_kernel(tc, x_seq, Wc, bc, Wg, bg, out):
             sm_of[b] = sm
 
         def soft_recip(b):
-            rs = smp.tile([P, 2, 16], F32, tag="rs", bufs=2)
+            rs = smp.tile([P, 2, 16], F32, tag="rs", bufs=3)
             nc.vector.reciprocal(out=rs[:].rearrange("p h j -> p (h j)"), in_=sm_of[b][:].rearrange("p a b -> p (a b)"))
             rs_of[b] = rs
 
@@ -261,25 +268,24 @@ def tile_dynamixerblock_pa_t_kernel(tc, x_seq, Wc, bc, Wg, bg, out):
         def has(i, n):
             return 0 <= i < n
 
-        for q in range(-1, N_BANKS + 6):
+        for q in range(-1, N_BANKS + 7):
             if has(q + PREFETCH, N_UNITS) and q >= 0:
                 load(q + PREFETCH)
             if has(q + 1, N_UNITS):
                 transposes(q + 1)
             if q == -1:
                 wg_transposes(0)
-            if has(q - 5, N_BANKS):
-                soft_sum(q - 5)
             if has(q - 4, N_BANKS):
                 soft_max(q - 4)
-            if has(q - 5, N_BANKS):
-                soft_recip(q - 5)
-            if has(q - 3, N_BANKS):
-                soft_bias(q - 3)
-            if has(q - 4, N_BANKS):
                 soft_sub(q - 4)
             if has(q - 5, N_BANKS):
-                soft_norm_store(q - 5)
+                soft_sum(q - 5)
+            if has(q - 3, N_BANKS):
+                soft_bias(q - 3)
+            if has(q - 5, N_BANKS):
+                soft_recip(q - 5)
+            if has(q - 6, N_BANKS):
+                soft_norm_store(q - 6)
             if q == 1:
                 wg_regroup(1)
             xg = regroup(q + 1) if has(q + 1, N_UNITS) else None
@@ -289,14 +295,15 @@ def tile_dynamixerblock_pa_t_kernel(tc, x_seq, Wc, bc, Wg, bg, out):
                 stage2(q - 2)
             if q == 0:
                 wg_transposes(1)
-            vg = bias_round(q) if has(q, N_UNITS) else None
+            if has(q, N_UNITS):
+                bias_round(q)
             if xg is not None:
                 quantise_x(q + 1, xg)
             if q == -1:
                 wg_regroup(0)
             if has(q - 4, N_BANKS):
                 soft_exp(q - 4)
-            if vg is not None:
-                quantise_v(q, vg)
+            if has(q, N_UNITS) and q % 2 == 1:
+                quantise_v(q // 2)
             if q == 0 or q == 1:
                 wg_finish(q)

@@ -80,6 +80,7 @@ def tile_dynamixerblock_pa_t_kernel(tc, x_seq, Wc, bc, Wg, bg, out):
         make_identity(nc, ident_f[:])
         ident_b = const.tile([P, P], BF16, tag="ident_b")
         make_identity(nc, ident_b[:])
+        perm_b = const.tile([P, P], BF16, tag="perm_b")
 
         wbd = const.tile([P, 4, 1024], U32, tag="wbd", align_bytes=64)
         wbds = const.tile([P, 4, 512], U8, tag="wbds", align_bytes=64)
@@ -89,6 +90,8 @@ def tile_dynamixerblock_pa_t_kernel(tc, x_seq, Wc, bc, Wg, bg, out):
         nc.vector.tensor_copy(out=perm_f[:].rearrange("p (a n) -> p a n", a=2),
                               in_=ident_f[:].rearrange("p (n a) -> p a n", a=2))
 
+        nc.vector.tensor_copy(out=perm_b[:].rearrange("p (j i b) -> p j i b", j=8, i=8, b=2),
+                              in_=ident_b[:].rearrange("p (i j b) -> p j i b", j=8, i=8, b=2))
         bct = const.tile([P, 2], F32, tag="bct")
         nc.vector.tensor_copy(out=bct[:], in_=bc_b[:])
         bgb = const.tile([P, 256], F32, tag="bgb")
@@ -124,14 +127,15 @@ def tile_dynamixerblock_pa_t_kernel(tc, x_seq, Wc, bc, Wg, bg, out):
                 wgp = ps_2.tile([P, 4, 256], BF16, tag="s2")
                 for t in range(4):
                     for a in range(2):
-                        nc.tensor.transpose(wgp[:, t, a * P:(a + 1) * P], wdup[:, a, 4 * lg + t, :], ident_b[:])
+                        nc.tensor.transpose(
+                            wgp[:, t, :].rearrange("p (j a w) -> p j a w", j=8, a=2, w=16)[:, :, a, :],
+                            wdup[:, a, 4 * lg + t, :], perm_b[:])
                 wgp_of[lg] = wgp
 
         def wg_regroup(pair):
+            copy = nc.vector.tensor_copy if pair == 0 else nc.scalar.copy
             for lg in (2 * pair, 2 * pair + 1):
-                dst = wgg[:, lg, :, :].rearrange("p (a i b) t -> p a i b t", a=8, i=16, b=2)
-                src = wgp_of[lg][:].rearrange("p t (i a b) -> p a i b t", a=8, i=16, b=2)
-                nc.vector.tensor_copy(out=dst, in_=src)
+                copy(out=wgg[:, lg, :, :], in_=wgp_of[lg][:].rearrange("p t c -> p c t"))
 
         def wg_finish(pair):
             two = slice(2 * pair, 2 * pair + 2)
@@ -254,8 +258,9 @@ def tile_dynamixerblock_pa_t_kernel(tc, x_seq, Wc, bc, Wg, bg, out):
 
         def soft_norm_store(b):
             oo = smp.tile([P, 2, 16, 16], F32, tag="oo", bufs=3)
+            eng = nc.gpsimd if N_BANKS - 4 <= b < N_BANKS - 1 else nc.vector
             for h in range(2):
-                nc.vector.tensor_tensor(
+                eng.tensor_tensor(
                     out=oo[:, h, :, :].rearrange("p i (a b) -> p i a b", b=2),
                     in0=dd_of[b][:, h * 256:(h + 1) * 256].rearrange("p (a i b) -> p i a b", a=8, i=16, b=2),
                     in1=rs_of[b][:, h, :].rearrange("p (a b) -> p a b", b=2).unsqueeze(1).to_broadcast([P, 16, 8, 2]),

@@ -150,19 +150,27 @@ def tile_dynamixerblock_pa_t_kernel(tc, x_seq, Wc, bc, Wg, bg, out):
         def transposes(k):
             xs32 = xs_of[k][:].bitcast(F32)
             banks = []
-            for t in range(4):
-                bank = ps_t.tile([P, 4, P], F32, tag="xt")
-                for c in range(4):
-                    nc.tensor.transpose(bank[:, c, :], xs32[:, t, c * P:(c + 1) * P], perm_f[:])
-                banks.append(bank)
+            for tp in range(2):
+                pair = []
+                for g in range(2):
+                    bank = ps_t.tile([P, 4, P], F32, tag="xt")
+                    for t in range(2):
+                        for u in range(2):
+                            c = 2 * g + u
+                            nc.tensor.transpose(bank[:, 2 * t + u, :],
+                                                xs32[:, 2 * tp + t, c * P:(c + 1) * P], perm_f[:])
+                    pair.append(bank)
+                banks.append(pair)
             bank_of[k] = banks
 
         def regroup(k):
             xg = xgp.tile([P, 4096], BF16, tag="xg", align_bytes=64)
             xg32 = xg[:].bitcast(F32).rearrange("p (g t n u) -> p g t n u", g=2, t=4, n=P, u=2)
-            for t in range(4):
-                copy = nc.vector.tensor_copy if (k == 0 and t % 2 == 1) else nc.scalar.copy
-                copy(out=xg32[:, :, t, :, :], in_=bank_of[k][t][:].rearrange("p (g u) n -> p g n u", g=2))
+            for tp in range(2):
+                for g in range(2):
+                    copy = nc.vector.tensor_copy if (k == 0 and g == 1) else nc.scalar.copy
+                    copy(out=xg32[:, g, 2 * tp:2 * tp + 2, :, :],
+                         in_=bank_of[k][tp][g][:].rearrange("p (t u) n -> p t n u", t=2))
             return xg
 
         def quantise_x(k, xg):

@@ -18,7 +18,8 @@ FLOPS = 2 * 8192 * 1024 * 256 + 2 * 4096 * 512 * 256
 
 N_UNITS = 16
 N_BANKS = 16
-PREFETCH = 3
+PREFETCH = 5
+QUARTERS = ((0, 0), (0, 1), (1, 0), (1, 1))
 
 
 def tile_dynamixerblock_pa_t_kernel(tc, x_seq, Wc, bc, Wg, bg, out):
@@ -28,7 +29,7 @@ def tile_dynamixerblock_pa_t_kernel(tc, x_seq, Wc, bc, Wg, bg, out):
     with ExitStack() as ctx:
         const = ctx.enter_context(tc.tile_pool(name="const", bufs=1))
         xin = ctx.enter_context(tc.tile_pool(name="xin", bufs=5))
-        xgp = ctx.enter_context(tc.tile_pool(name="xgp", bufs=2))
+        xgp = ctx.enter_context(tc.tile_pool(name="xgp", bufs=3))
         xwp = ctx.enter_context(tc.tile_pool(name="xwp", bufs=3))
         vgp = ctx.enter_context(tc.tile_pool(name="vgp", bufs=3))
         vwp = ctx.enter_context(tc.tile_pool(name="vwp", bufs=3))
@@ -47,13 +48,14 @@ def tile_dynamixerblock_pa_t_kernel(tc, x_seq, Wc, bc, Wg, bg, out):
         sm_of = {}
         wgp_of = {}
         tt_of = {}
+        oo_of = {}
+        xg_of = {}
         vg_of = {}
         mx_of = {}
         dd_of = {}
         rs_of = {}
 
         wc_sb = const.tile([P, 2, 1024], BF16, tag="wc_sb")
-        nc.sync.dma_start(out=wc_sb[:], in_=Wc.rearrange("(h p) k -> p h k", p=P))
         wg_sb = const.tile([P, 2, 512], BF16, tag="wg_sb")
         nc.scalar.dma_start(out=wg_sb[:], in_=Wg.rearrange("(a p) k -> p a k", p=P))
         bc_b = const.tile([P, 2], BF16, tag="bc_b")
@@ -73,7 +75,9 @@ def tile_dynamixerblock_pa_t_kernel(tc, x_seq, Wc, bc, Wg, bg, out):
                 nc.sync.dma_start(out=xs[:], in_=src)
             xs_of[k] = xs
 
-        for k in range(PREFETCH):
+        load(0)
+        nc.sync.dma_start(out=wc_sb[:], in_=Wc.rearrange("(h p) k -> p h k", p=P))
+        for k in range(1, PREFETCH):
             load(k)
 
         ident_f = const.tile([P, P], F32, tag="ident_f")
@@ -82,60 +86,65 @@ def tile_dynamixerblock_pa_t_kernel(tc, x_seq, Wc, bc, Wg, bg, out):
         make_identity(nc, ident_b[:])
         perm_b = const.tile([P, P], BF16, tag="perm_b")
 
-        wbd = const.tile([P, 4, 1024], U32, tag="wbd", align_bytes=64)
-        wbds = const.tile([P, 4, 512], U8, tag="wbds", align_bytes=64)
-        nc.vector.memset(wbd[:].bitcast(I32), 0)
-        nc.vector.memset(wbds[:].bitcast(I32), 0)
         perm_f = const.tile([P, P], F32, tag="perm_f")
         nc.vector.tensor_copy(out=perm_f[:].rearrange("p (a n) -> p a n", a=2),
                               in_=ident_f[:].rearrange("p (n a) -> p a n", a=2))
 
         nc.vector.tensor_copy(out=perm_b[:].rearrange("p (j i b) -> p j i b", j=8, i=8, b=2),
                               in_=ident_b[:].rearrange("p (i j b) -> p j i b", j=8, i=8, b=2))
+        wbd = const.tile([P, 4, 1024], U32, tag="wbd", align_bytes=64)
+        wbds = const.tile([P, 4, 512], U8, tag="wbds", align_bytes=64)
+        nc.vector.memset(wbd[:].bitcast(I32), 0)
+        nc.gpsimd.memset(wbds[:].bitcast(I32), 0)
         bct = const.tile([P, 2], F32, tag="bct")
-        nc.vector.tensor_copy(out=bct[:], in_=bc_b[:])
         bgb = const.tile([P, 256], F32, tag="bgb")
-        nc.vector.tensor_copy(out=bgb[:].rearrange("p (a i b) -> p a i b", a=8, i=16, b=2),
-                              in_=bg_b[:].rearrange("p (i a b) -> p a i b", a=8, i=16, b=2))
+
+        def biases():
+            nc.vector.tensor_copy(out=bct[:], in_=bc_b[:])
+            nc.vector.tensor_copy(out=bgb[:].rearrange("p (a i b) -> p a i b", a=8, i=16, b=2),
+                                  in_=bg_b[:].rearrange("p (i a b) -> p a i b", a=8, i=16, b=2))
 
         wcg = const.tile([P, 2048], BF16, tag="wcg", align_bytes=64)
-        wcg32 = wcg[:].bitcast(F32).rearrange("p (g h m u) -> p g h m u", g=2, h=2, m=P, u=2)
-        wc32 = wc_sb[:].bitcast(F32)
-        for hh in range(2):
-            wbank = ps_t.tile([P, 4, P], F32, tag="xt")
-            for c in range(4):
-                nc.tensor.transpose(wbank[:, c, :], wc32[:, hh, c * P:(c + 1) * P], ident_f[:])
-            nc.scalar.copy(out=wcg32[:, :, hh, :, :],
-                           in_=wbank[:].rearrange("p (g u) m -> p g m u", g=2))
         wcw = const.tile([P, 512], U32, tag="wcw", align_bytes=64)
         wcs = const.tile([P, 512], U8, tag="wcs", align_bytes=64)
-        nc.vector.quantize_mx(out=wcw[:].bitcast(FP8X4), scales=wcs[:], in_=wcg[:])
+        wc_banks = []
+
+        def wc_transposes():
+            wc32 = wc_sb[:].bitcast(F32)
+            for hh in range(2):
+                wbank = ps_1.tile([P, 4, P], F32, tag="s1")
+                for c in range(4):
+                    nc.tensor.transpose(wbank[:, c, :], wc32[:, hh, c * P:(c + 1) * P], ident_f[:])
+                wc_banks.append(wbank)
+
+        def wc_regroup():
+            wcg32 = wcg[:].bitcast(F32).rearrange("p (g h m u) -> p g h m u", g=2, h=2, m=P, u=2)
+            for hh in range(2):
+                nc.scalar.copy(out=wcg32[:, :, hh, :, :],
+                               in_=wc_banks[hh][:].rearrange("p (g u) m -> p g m u", g=2))
+
+        def wc_quantise():
+            nc.vector.quantize_mx(out=wcw[:].bitcast(FP8X4), scales=wcs[:], in_=wcg[:])
 
         wdup = const.tile([P, 2, 16, P], BF16, tag="wdup")
-        nc.vector.tensor_copy(
-            out=wdup[:, 0, :, :].rearrange("p l (d r) -> p l d r", d=4),
-            in_=wg_sb[:, 0, :].rearrange("p (l r) -> p l r", r=32).unsqueeze(2).to_broadcast([P, 16, 4, 32]))
-        nc.gpsimd.tensor_scalar(
-            out=wdup[:, 1, :, :].rearrange("p l (d r) -> p l d r", d=4),
-            in0=wg_sb[:, 1, :].rearrange("p (l r) -> p l r", r=32).unsqueeze(2).to_broadcast([P, 16, 4, 32]),
-            scalar1=1.0, scalar2=0.0, op0=ALU.mult, op1=ALU.add)
+        for a in range(2):
+            nc.vector.tensor_copy(
+                out=wdup[:, a, :, :].rearrange("p l (d r) -> p l d r", d=4),
+                in_=wg_sb[:, a, :].rearrange("p (l r) -> p l r", r=32).unsqueeze(2).to_broadcast([P, 16, 4, 32]))
         wgg = const.tile([P, 4, 256, 4], BF16, tag="wgg", align_bytes=64)
         wgw = const.tile([P, 4, 256], U32, tag="wgw", align_bytes=64)
 
-        def wg_transposes(pair):
-            for lg in (2 * pair, 2 * pair + 1):
-                wgp = ps_2.tile([P, 4, 256], BF16, tag="s2")
-                for t in range(4):
-                    for a in range(2):
-                        nc.tensor.transpose(
-                            wgp[:, t, :].rearrange("p (j a w) -> p j a w", j=8, a=2, w=16)[:, :, a, :],
-                            wdup[:, a, 4 * lg + t, :], perm_b[:])
-                wgp_of[lg] = wgp
+        def wg_transposes(lg):
+            wgp = ps_2.tile([P, 4, 256], BF16, tag="s2")
+            for t in range(4):
+                for a in range(2):
+                    nc.tensor.transpose(
+                        wgp[:, t, :].rearrange("p (j a w) -> p j a w", j=8, a=2, w=16)[:, :, a, :],
+                        wdup[:, a, 4 * lg + t, :], perm_b[:])
+            wgp_of[lg] = wgp
 
-        def wg_regroup(pair):
-            copy = nc.vector.tensor_copy if pair == 0 else nc.scalar.copy
-            for lg in (2 * pair, 2 * pair + 1):
-                copy(out=wgg[:, lg, :, :], in_=wgp_of[lg][:].rearrange("p t c -> p c t"))
+        def wg_regroup(lg, copy):
+            copy(out=wgg[:, lg, :, :], in_=wgp_of[lg][:].rearrange("p t c -> p c t"))
 
         def wg_finish(pair):
             two = slice(2 * pair, 2 * pair + 2)
@@ -143,15 +152,13 @@ def tile_dynamixerblock_pa_t_kernel(tc, x_seq, Wc, bc, Wg, bg, out):
                 nc.vector.quantize_mx(out=wgw[:, lg, :].bitcast(FP8X4), scales=wbds[:, lg, 0:256],
                                       in_=wgg[:, lg, :, :].rearrange("p c t -> p (c t)"))
             for d in range(4):
-                nc.vector.tensor_copy(out=wbd[32 * d:32 * d + 32, two, 256 * d:256 * d + 256].bitcast(I32),
-                                      in_=wgw[32 * d:32 * d + 32, two, :].bitcast(I32))
+                nc.sync.dma_start(out=wbd[32 * d:32 * d + 32, two, 256 * d:256 * d + 256].bitcast(I32),
+                                  in_=wgw[32 * d:32 * d + 32, two, :].bitcast(I32))
             nc.vector.tensor_copy(out=wbds[:, two, 256:512].bitcast(I32), in_=wbds[:, two, 0:256].bitcast(I32))
 
-        def transposes(k):
+        def transposes(k, tps=(0, 1)):
             xs32 = xs_of[k][:].bitcast(F32)
-            banks = []
-            for tp in range(2):
-                pair = []
+            for tp in tps:
                 for g in range(2):
                     bank = ps_t.tile([P, 4, P], F32, tag="xt")
                     for t in range(2):
@@ -159,21 +166,19 @@ def tile_dynamixerblock_pa_t_kernel(tc, x_seq, Wc, bc, Wg, bg, out):
                             c = 2 * g + u
                             nc.tensor.transpose(bank[:, 2 * t + u, :],
                                                 xs32[:, 2 * tp + t, c * P:(c + 1) * P], perm_f[:])
-                    pair.append(bank)
-                banks.append(pair)
-            bank_of[k] = banks
+                    bank_of[k, tp, g] = bank
 
-        def regroup(k):
-            xg = xgp.tile([P, 4096], BF16, tag="xg", align_bytes=64)
-            xg32 = xg[:].bitcast(F32).rearrange("p (g t n u) -> p g t n u", g=2, t=4, n=P, u=2)
-            for tp in range(2):
-                for g in range(2):
-                    copy = nc.vector.tensor_copy if (k == 0 and g == 1) else nc.scalar.copy
-                    copy(out=xg32[:, g, 2 * tp:2 * tp + 2, :, :],
-                         in_=bank_of[k][tp][g][:].rearrange("p (t u) n -> p t n u", t=2))
-            return xg
+        def regroup(k, pieces, copy):
+            if k not in xg_of:
+                xg_new = xgp.tile([P, 4096], BF16, tag="xg", align_bytes=64)
+                xg_of[k] = xg_new
+            xg32 = xg_of[k][:].bitcast(F32).rearrange("p (g t n u) -> p g t n u", g=2, t=4, n=P, u=2)
+            for tp, g in pieces:
+                copy(out=xg32[:, g, 2 * tp:2 * tp + 2, :, :],
+                     in_=bank_of[k, tp, g][:].rearrange("p (t u) n -> p t n u", t=2))
 
-        def quantise_x(k, xg):
+        def quantise_x(k):
+            xg = xg_of[k]
             xw = xwp.tile([P, 1024], U32, tag="xw", align_bytes=64)
             xsc = xwp.tile([P, 1024], U8, tag="xsc", align_bytes=64)
             nc.vector.quantize_mx(out=xw[:].bitcast(FP8X4), scales=xsc[:], in_=xg[:])
@@ -233,20 +238,19 @@ def tile_dynamixerblock_pa_t_kernel(tc, x_seq, Wc, bc, Wg, bg, out):
             return ap.rearrange("p (a i b) -> p a b i", a=16, i=16, b=2)
 
         def soft_bias(b):
-            tt = smp.tile([P, 512], F32, tag="tt", bufs=3)
+            tt = smp.tile([P, 512], F32, tag="tt", bufs=4)
             nc.vector.tensor_tensor(out=tt[:].rearrange("p (h c) -> p h c", h=2),
                                     in0=acc2_of[b][:].rearrange("p (h c) -> p h c", h=2),
                                     in1=bgb[:].unsqueeze(1).to_broadcast([P, 2, 256]), op=ALU.add)
             tt_of[b] = tt
 
         def soft_max(b):
-            mx = smp.tile([P, 16, 2], F32, tag="mx", bufs=2)
+            mx = smp.tile([P, 16, 2], F32, tag="mx", bufs=4)
             nc.vector.tensor_reduce(out=mx[:], in_=by_abi(tt_of[b][:]), axis=AX.X, op=ALU.max)
             mx_of[b] = mx
 
-        def soft_sub(b):
-            dd = smp.tile([P, 512], F32, tag="dd", bufs=4)
-            eng = nc.vector if b >= N_BANKS - 2 else nc.gpsimd
+        def soft_sub(b, eng):
+            dd = smp.tile([P, 512], F32, tag="dd", bufs=5)
             eng.tensor_tensor(out=by_aib(dd[:]), in0=by_aib(tt_of[b][:]),
                                     in1=mx_of[b][:].unsqueeze(2).to_broadcast([P, 16, 16, 2]), op=ALU.subtract)
             dd_of[b] = dd
@@ -255,68 +259,130 @@ def tile_dynamixerblock_pa_t_kernel(tc, x_seq, Wc, bc, Wg, bg, out):
             nc.scalar.activation(out=dd_of[b][:], in_=dd_of[b][:], func=ACTF.Exp)
 
         def soft_sum(b):
-            sm = smp.tile([P, 16, 2], F32, tag="sm", bufs=2)
+            sm = smp.tile([P, 16, 2], F32, tag="sm", bufs=3)
             nc.vector.tensor_reduce(out=sm[:], in_=by_abi(dd_of[b][:]), axis=AX.X, op=ALU.add)
             sm_of[b] = sm
 
         def soft_recip(b):
-            rs = smp.tile([P, 2, 16], F32, tag="rs", bufs=3)
+            rs = smp.tile([P, 2, 16], F32, tag="rs", bufs=4)
             nc.vector.reciprocal(out=rs[:].rearrange("p h j -> p (h j)"), in_=sm_of[b][:].rearrange("p a b -> p (a b)"))
             rs_of[b] = rs
 
-        def soft_norm_store(b):
-            oo = smp.tile([P, 2, 16, 16], F32, tag="oo", bufs=3)
-            eng = nc.gpsimd if N_BANKS - 4 <= b < N_BANKS - 1 else nc.vector
-            for h in range(2):
+        def soft_norm(b, heads, eng):
+            if b not in oo_of:
+                oo_new = smp.tile([P, 2, 16, 16], F32, tag="oo", bufs=4)
+                oo_of[b] = oo_new
+            for h in heads:
                 eng.tensor_tensor(
-                    out=oo[:, h, :, :].rearrange("p i (a b) -> p i a b", b=2),
+                    out=oo_of[b][:, h, :, :].rearrange("p i (a b) -> p i a b", b=2),
                     in0=dd_of[b][:, h * 256:(h + 1) * 256].rearrange("p (a i b) -> p i a b", a=8, i=16, b=2),
                     in1=rs_of[b][:, h, :].rearrange("p (a b) -> p a b", b=2).unsqueeze(1).to_broadcast([P, 16, 8, 2]),
                     op=ALU.mult)
+
+        def store(b):
             ng, half = divmod(b, 2)
             for hh in range(2):
                 nc.sync.dma_start(out=out_rows[ng, hh][:, half * 512:(half + 1) * 512],
-                                  in_=oo[hh * 64:(hh + 1) * 64].rearrange("p h i j -> p (h i j)"))
+                                  in_=oo_of[b][hh * 64:(hh + 1) * 64].rearrange("p h i j -> p (h i j)"))
 
         def has(i, n):
             return 0 <= i < n
 
-        for q in range(-1, N_BANKS + 7):
-            if has(q + PREFETCH, N_UNITS) and q >= 0:
-                load(q + PREFETCH)
+        transposes(0, [0])
+        transposes(0, [1])
+        wg_transposes(0)
+        wg_transposes(1)
+        regroup(0, [(0, 0), (1, 0)], nc.scalar.copy)
+        regroup(0, [(0, 1), (1, 1)], nc.vector.tensor_copy)
+        wc_transposes()
+        wg_regroup(0, nc.scalar.copy)
+        wc_regroup()
+        biases()
+        quantise_x(0)
+        wg_regroup(1, nc.scalar.copy)
+        wc_quantise()
+        wg_transposes(2)
+        wg_transposes(3)
+        wg_finish(0)
+        transposes(1)
+        regroup(1, [(0, 0), (1, 0)], nc.scalar.copy)
+        regroup(1, [(0, 1), (1, 1)], nc.vector.tensor_copy)
+        stage1(0)
+        wg_regroup(2, nc.scalar.copy)
+        wg_regroup(3, nc.vector.tensor_copy)
+        bias_round(0)
+        quantise_x(1)
+        wg_finish(1)
+
+        for q in range(1, N_UNITS):
+            if has(q + 4, N_UNITS):
+                load(q + 4)
             if has(q + 1, N_UNITS):
                 transposes(q + 1)
-            if q == -1:
-                wg_transposes(0)
             if has(q - 4, N_BANKS):
                 soft_max(q - 4)
-                soft_sub(q - 4)
+                soft_sub(q - 4, nc.gpsimd)
             if has(q - 5, N_BANKS):
                 soft_sum(q - 5)
             if has(q - 3, N_BANKS):
                 soft_bias(q - 3)
             if has(q - 5, N_BANKS):
                 soft_recip(q - 5)
-            if has(q - 6, N_BANKS):
-                soft_norm_store(q - 6)
-            if q == 1:
-                wg_regroup(1)
-            xg = regroup(q + 1) if has(q + 1, N_UNITS) else None
+            if has(q + 1, N_UNITS):
+                mine = [(1, 1)] if q < 4 else []
+                regroup(q + 1, [piece for piece in QUARTERS if piece not in mine], nc.scalar.copy)
+                regroup(q + 1, mine, nc.vector.tensor_copy)
             if has(q, N_UNITS):
                 stage1(q)
             if has(q - 2, N_BANKS):
                 stage2(q - 2)
-            if q == 0:
-                wg_transposes(1)
             if has(q, N_UNITS):
                 bias_round(q)
-            if xg is not None:
-                quantise_x(q + 1, xg)
-            if q == -1:
-                wg_regroup(0)
+            if has(q + 1, N_UNITS):
+                quantise_x(q + 1)
             if has(q - 4, N_BANKS):
                 soft_exp(q - 4)
-            if has(q, N_UNITS) and q % 2 == 1:
+            if q % 2 == 1 and q < N_UNITS - 1:
                 quantise_v(q // 2)
-            if q == 0 or q == 1:
-                wg_finish(q)
+            if has(q - 5, N_BANKS):
+                soft_norm(q - 5, [0, 1], nc.vector)
+                store(q - 5)
+            if q == N_UNITS - 1:
+                quantise_v(q // 2)
+        stage2(14)
+        soft_bias(13)
+        stage2(15)
+        soft_max(12)
+        soft_sub(12, nc.gpsimd)
+        soft_exp(12)
+        soft_max(13)
+        soft_sub(13, nc.gpsimd)
+        soft_exp(13)
+        soft_sum(11)
+        soft_bias(14)
+        soft_recip(11)
+        soft_bias(15)
+        soft_max(14)
+        soft_sub(14, nc.gpsimd)
+        soft_exp(14)
+        soft_norm(11, [0, 1], nc.vector)
+        store(11)
+        soft_sum(12)
+        soft_max(15)
+        soft_sub(15, nc.gpsimd)
+        soft_exp(15)
+        soft_recip(12)
+        soft_sum(13)
+        soft_norm(12, [0, 1], nc.vector)
+        store(12)
+        soft_recip(13)
+        soft_sum(14)
+        soft_norm(13, [0, 1], nc.vector)
+        store(13)
+        soft_recip(14)
+        soft_sum(15)
+        soft_norm(14, [0, 1], nc.vector)
+        store(14)
+        soft_recip(15)
+        soft_norm(15, [0, 1], nc.vector)
+        store(15)

@@ -319,9 +319,14 @@ def tile_dynamixerblock_pa_t_kernel(tc, x_seq, Wc, bc, Wg, bg, out):
                 load(q + 4)
             if has(q + 1, N_UNITS):
                 transposes(q + 1)
+            if has(q - 6, N_BANKS):
+                soft_norm(q - 6, [0], nc.vector)
             if has(q - 4, N_BANKS):
                 soft_max(q - 4)
                 soft_sub(q - 4, nc.gpsimd)
+            if has(q - 6, N_BANKS):
+                soft_norm(q - 6, [1], nc.vector)
+                store(q - 6)
             if has(q - 5, N_BANKS):
                 soft_sum(q - 5)
             if has(q - 3, N_BANKS):
@@ -344,11 +349,10 @@ def tile_dynamixerblock_pa_t_kernel(tc, x_seq, Wc, bc, Wg, bg, out):
                 soft_exp(q - 4)
             if q % 2 == 1 and q < N_UNITS - 1:
                 quantise_v(q // 2)
-            if has(q - 5, N_BANKS):
-                soft_norm(q - 5, [0, 1], nc.vector)
-                store(q - 5)
             if q == N_UNITS - 1:
                 quantise_v(q // 2)
+        soft_norm(10, [0, 1], nc.vector)
+        store(10)
         stage2(14)
         soft_bias(13)
         stage2(15)

from contextlib import ExitStack

import concourse.mybir as mybir
from concourse.masks import make_identity

F32 = mybir.dt.float32
BF16 = mybir.dt.bfloat16
U32 = mybir.dt.uint32
U8 = mybir.dt.uint8
I32 = mybir.dt.int32
FP8X4 = mybir.dt.float8_e4m3fn_x4
ALU = mybir.AluOpType
ACTF = mybir.ActivationFunctionType
AX = mybir.AxisListType

P = 128
FLOPS = 2 * 8192 * 1024 * 256 + 2 * 4096 * 512 * 256

N_UNITS = 16
N_BANKS = 16
PREFETCH = 5
QUARTERS = ((0, 0), (0, 1), (1, 0), (1, 1))


def tile_dynamixerblock_pa_t_kernel(tc, x_seq, Wc, bc, Wg, bg, out):
    nc = tc.nc
    x_rows = x_seq.rearrange("n (a b) c -> (n a) b c", a=2)
    out_rows = out.rearrange("(g n) (hh q) i j -> g hh n (q i j)", n=64, hh=2)
    with ExitStack() as ctx:
        const = ctx.enter_context(tc.tile_pool(name="const", bufs=1))
        xin = ctx.enter_context(tc.tile_pool(name="xin", bufs=5))
        xgp = ctx.enter_context(tc.tile_pool(name="xgp", bufs=3))
        xwp = ctx.enter_context(tc.tile_pool(name="xwp", bufs=3))
        vgp = ctx.enter_context(tc.tile_pool(name="vgp", bufs=3))
        vwp = ctx.enter_context(tc.tile_pool(name="vwp", bufs=3))
        smp = ctx.enter_context(tc.tile_pool(name="smp", bufs=3))
        ps_t = ctx.enter_context(tc.psum_pool(name="ps_t", bufs=4))
        ps_1 = ctx.enter_context(tc.psum_pool(name="ps_1", bufs=2))
        ps_2 = ctx.enter_context(tc.psum_pool(name="ps_2", bufs=2))
        ctx.enter_context(tc.manual_schedule())

        xs_of = {}
        bank_of = {}
        xw_of = {}
        acc1_of = {}
        vw_of = {}
        acc2_of = {}
        sm_of = {}
        wgp_of = {}
        tt_of = {}
        oo_of = {}
        xg_of = {}
        vg_of = {}
        mx_of = {}
        dd_of = {}
        rs_of = {}

        wc_sb = const.tile([P, 2, 1024], BF16, tag="wc_sb")
        wg_sb = const.tile([P, 2, 512], BF16, tag="wg_sb")
        nc.scalar.dma_start(out=wg_sb[:], in_=Wg.rearrange("(a p) k -> p a k", p=P))
        bc_b = const.tile([P, 2], BF16, tag="bc_b")
        with nc.allow_non_contiguous_dma(reason="256 bias values, one per partition"):
            nc.scalar.dma_start(out=bc_b[:], in_=bc.rearrange("(h p) -> p h", p=P))
        bg_b = const.tile([P, 256], BF16, tag="bg_b")
        nc.scalar.dma_start(out=bg_b[:], in_=bg.partition_broadcast(P))

        def load(k):
            ng, bq = divmod(k, 2)
            xs = xin.tile([P, 4, 1024], BF16, tag="xs")
            src = x_rows[ng * P:(ng + 1) * P, 4 * bq:4 * bq + 4, :]
            if k == 0:
                for t in range(4):
                    nc.sync.dma_start(out=xs[:, t, :], in_=src[:, t, :])
            else:
                nc.sync.dma_start(out=xs[:], in_=src)
            xs_of[k] = xs

        load(0)
        nc.sync.dma_start(out=wc_sb[:], in_=Wc.rearrange("(h p) k -> p h k", p=P))
        for k in range(1, PREFETCH):
            load(k)

        ident_f = const.tile([P, P], F32, tag="ident_f")
        make_identity(nc, ident_f[:])
        ident_b = const.tile([P, P], BF16, tag="ident_b")
        make_identity(nc, ident_b[:])
        perm_b = const.tile([P, P], BF16, tag="perm_b")

        perm_f = const.tile([P, P], F32, tag="perm_f")
        nc.vector.tensor_copy(out=perm_f[:].rearrange("p (a n) -> p a n", a=2),
                              in_=ident_f[:].rearrange("p (n a) -> p a n", a=2))

        nc.vector.tensor_copy(out=perm_b[:].rearrange("p (j i b) -> p j i b", j=8, i=8, b=2),
                              in_=ident_b[:].rearrange("p (i j b) -> p j i b", j=8, i=8, b=2))
        wbd = const.tile([P, 4, 1024], U32, tag="wbd", align_bytes=64)
        wbds = const.tile([P, 4, 512], U8, tag="wbds", align_bytes=64)
        nc.vector.memset(wbd[:].bitcast(I32), 0)
        nc.gpsimd.memset(wbds[:].bitcast(I32), 0)
        bct = const.tile([P, 2], F32, tag="bct")
        bgb = const.tile([P, 256], F32, tag="bgb")

        def biases():
            nc.vector.tensor_copy(out=bct[:], in_=bc_b[:])
            nc.vector.tensor_copy(out=bgb[:].rearrange("p (a i b) -> p a i b", a=8, i=16, b=2),
                                  in_=bg_b[:].rearrange("p (i a b) -> p a i b", a=8, i=16, b=2))

        wcg = const.tile([P, 2048], BF16, tag="wcg", align_bytes=64)
        wcw = const.tile([P, 512], U32, tag="wcw", align_bytes=64)
        wcs = const.tile([P, 512], U8, tag="wcs", align_bytes=64)
        wc_banks = []

        def wc_transposes():
            wc32 = wc_sb[:].bitcast(F32)
            for hh in range(2):
                wbank = ps_1.tile([P, 4, P], F32, tag="s1")
                for c in range(4):
                    nc.tensor.transpose(wbank[:, c, :], wc32[:, hh, c * P:(c + 1) * P], ident_f[:])
                wc_banks.append(wbank)

        def wc_regroup():
            wcg32 = wcg[:].bitcast(F32).rearrange("p (g h m u) -> p g h m u", g=2, h=2, m=P, u=2)
            for hh in range(2):
                nc.scalar.copy(out=wcg32[:, :, hh, :, :],
                               in_=wc_banks[hh][:].rearrange("p (g u) m -> p g m u", g=2))

        def wc_quantise():
            nc.vector.quantize_mx(out=wcw[:].bitcast(FP8X4), scales=wcs[:], in_=wcg[:])

        wdup = const.tile([P, 2, 16, P], BF16, tag="wdup")
        for a in range(2):
            nc.vector.tensor_copy(
                out=wdup[:, a, :, :].rearrange("p l (d r) -> p l d r", d=4),
                in_=wg_sb[:, a, :].rearrange("p (l r) -> p l r", r=32).unsqueeze(2).to_broadcast([P, 16, 4, 32]))
        wgg = const.tile([P, 4, 256, 4], BF16, tag="wgg", align_bytes=64)
        wgw = const.tile([P, 4, 256], U32, tag="wgw", align_bytes=64)

        def wg_transposes(lg):
            wgp = ps_2.tile([P, 4, 256], BF16, tag="s2")
            for t in range(4):
                for a in range(2):
                    nc.tensor.transpose(
                        wgp[:, t, :].rearrange("p (j a w) -> p j a w", j=8, a=2, w=16)[:, :, a, :],
                        wdup[:, a, 4 * lg + t, :], perm_b[:])
            wgp_of[lg] = wgp

        def wg_regroup(lg, copy):
            copy(out=wgg[:, lg, :, :], in_=wgp_of[lg][:].rearrange("p t c -> p c t"))

        def wg_finish(pair):
            two = slice(2 * pair, 2 * pair + 2)
            for lg in (2 * pair, 2 * pair + 1):
                nc.vector.quantize_mx(out=wgw[:, lg, :].bitcast(FP8X4), scales=wbds[:, lg, 0:256],
                                      in_=wgg[:, lg, :, :].rearrange("p c t -> p (c t)"))
            for d in range(4):
                nc.sync.dma_start(out=wbd[32 * d:32 * d + 32, two, 256 * d:256 * d + 256].bitcast(I32),
                                  in_=wgw[32 * d:32 * d + 32, two, :].bitcast(I32))
            nc.vector.tensor_copy(out=wbds[:, two, 256:512].bitcast(I32), in_=wbds[:, two, 0:256].bitcast(I32))

        def transposes(k, tps=(0, 1)):
            xs32 = xs_of[k][:].bitcast(F32)
            for tp in tps:
                for g in range(2):
                    bank = ps_t.tile([P, 4, P], F32, tag="xt")
                    for t in range(2):
                        for u in range(2):
                            c = 2 * g + u
                            nc.tensor.transpose(bank[:, 2 * t + u, :],
                                                xs32[:, 2 * tp + t, c * P:(c + 1) * P], perm_f[:])
                    bank_of[k, tp, g] = bank

        def regroup(k, pieces, copy):
            if k not in xg_of:
                xg_new = xgp.tile([P, 4096], BF16, tag="xg", align_bytes=64)
                xg_of[k] = xg_new
            xg32 = xg_of[k][:].bitcast(F32).rearrange("p (g t n u) -> p g t n u", g=2, t=4, n=P, u=2)
            for tp, g in pieces:
                copy(out=xg32[:, g, 2 * tp:2 * tp + 2, :, :],
                     in_=bank_of[k, tp, g][:].rearrange("p (t u) n -> p t n u", t=2))

        def quantise_x(k):
            xg = xg_of[k]
            xw = xwp.tile([P, 1024], U32, tag="xw", align_bytes=64)
            xsc = xwp.tile([P, 1024], U8, tag="xsc", align_bytes=64)
            nc.vector.quantize_mx(out=xw[:].bitcast(FP8X4), scales=xsc[:], in_=xg[:])
            xw_of[k] = (xw, xsc)

        def stage1(k):
            xw, xsc = xw_of[k]
            accs = []
            for hh in range(2):
                acc = ps_1.tile([P, 512], F32, tag="s1")
                for g in range(2):
                    w0 = (g * 2 + hh) * P
                    nc.tensor.matmul_mx(out=acc[:],
                                        lhsT=wcw[:, w0:w0 + P].bitcast(FP8X4), lhsT_scale=wcs[:, w0:w0 + P],
                                        rhs=xw[:, g * 512:(g + 1) * 512].bitcast(FP8X4),
                                        rhs_scale=xsc[:, g * 512:(g + 1) * 512],
                                        start=(g == 0), stop=(g == 1))
                accs.append(acc)
            acc1_of[k] = accs

        def bias_round(k):
            ng, bq = divmod(k, 2)
            if bq == 0:
                vg_new = vgp.tile([P, 2, 2, 2, 64, 4], BF16, tag="vg", align_bytes=64)
                vg_of[ng] = vg_new
            for hh in range(2):
                nc.scalar.activation(out=vg_of[ng][:, bq, :, hh, :, :],
                                     in_=acc1_of[k][hh][:].rearrange("p (t a n) -> p a n t", t=4, a=2),
                                     func=ACTF.Identity, bias=bct[:, hh:hh + 1], scale=1.0)

        def quantise_v(ng):
            vw = vwp.tile([P, 2, 256], U32, tag="vw", align_bytes=64)
            vsc = vwp.tile([P, 2, 256], U8, tag="vsc", align_bytes=64)
            nc.vector.quantize_mx(out=vw[:].rearrange("p q c -> p (q c)").bitcast(FP8X4),
                                  scales=vsc[:].rearrange("p q c -> p (q c)"),
                                  in_=vg_of[ng][:].rearrange("p q a h n t -> p (q a h n t)"))
            vw_of[ng] = (vw, vsc)

        def stage2(b):
            ng, half = divmod(b, 2)
            vw, vsc = vw_of[ng]
            acc2 = ps_2.tile([P, 512], F32, tag="s2")
            for i in range(4):
                bq, a = divmod(i, 2)
                nc.tensor.matmul_mx(out=acc2[:],
                                    lhsT=vw[:, bq, a * P:(a + 1) * P].bitcast(FP8X4),
                                    lhsT_scale=vsc[:, bq, a * P:(a + 1) * P],
                                    rhs=wbd[:, 2 * a + bq, half * 512:(half + 1) * 512].bitcast(FP8X4),
                                    rhs_scale=wbds[:, 2 * a + bq, :],
                                    start=(i == 0), stop=(i == 3))
            acc2_of[b] = acc2

        def by_aib(ap):
            return ap.rearrange("p (a i b) -> p a i b", a=16, i=16, b=2)

        def by_abi(ap):
            return ap.rearrange("p (a i b) -> p a b i", a=16, i=16, b=2)

        def soft_bias(b):
            tt = smp.tile([P, 512], F32, tag="tt", bufs=4)
            nc.vector.tensor_tensor(out=tt[:].rearrange("p (h c) -> p h c", h=2),
                                    in0=acc2_of[b][:].rearrange("p (h c) -> p h c", h=2),
                                    in1=bgb[:].unsqueeze(1).to_broadcast([P, 2, 256]), op=ALU.add)
            tt_of[b] = tt

        def soft_max(b):
            mx = smp.tile([P, 16, 2], F32, tag="mx", bufs=4)
            nc.vector.tensor_reduce(out=mx[:], in_=by_abi(tt_of[b][:]), axis=AX.X, op=ALU.max)
            mx_of[b] = mx

        def soft_sub(b, eng):
            dd = smp.tile([P, 512], F32, tag="dd", bufs=5)
            eng.tensor_tensor(out=by_aib(dd[:]), in0=by_aib(tt_of[b][:]),
                                    in1=mx_of[b][:].unsqueeze(2).to_broadcast([P, 16, 16, 2]), op=ALU.subtract)
            dd_of[b] = dd

        def soft_exp(b):
            nc.scalar.activation(out=dd_of[b][:], in_=dd_of[b][:], func=ACTF.Exp)

        def soft_sum(b):
            sm = smp.tile([P, 16, 2], F32, tag="sm", bufs=3)
            nc.vector.tensor_reduce(out=sm[:], in_=by_abi(dd_of[b][:]), axis=AX.X, op=ALU.add)
            sm_of[b] = sm

        def soft_recip(b):
            rs = smp.tile([P, 2, 16], F32, tag="rs", bufs=4)
            nc.vector.reciprocal(out=rs[:].rearrange("p h j -> p (h j)"), in_=sm_of[b][:].rearrange("p a b -> p (a b)"))
            rs_of[b] = rs

        def soft_norm(b, heads, eng):
            if b not in oo_of:
                oo_new = smp.tile([P, 2, 16, 16], F32, tag="oo", bufs=4)
                oo_of[b] = oo_new
            for h in heads:
                eng.tensor_tensor(
                    out=oo_of[b][:, h, :, :].rearrange("p i (a b) -> p i a b", b=2),
                    in0=dd_of[b][:, h * 256:(h + 1) * 256].rearrange("p (a i b) -> p i a b", a=8, i=16, b=2),
                    in1=rs_of[b][:, h, :].rearrange("p (a b) -> p a b", b=2).unsqueeze(1).to_broadcast([P, 16, 8, 2]),
                    op=ALU.mult)

        def store(b):
            ng, half = divmod(b, 2)
            for hh in range(2):
                nc.sync.dma_start(out=out_rows[ng, hh][:, half * 512:(half + 1) * 512],
                                  in_=oo_of[b][hh * 64:(hh + 1) * 64].rearrange("p h i j -> p (h i j)"))

        def has(i, n):
            return 0 <= i < n

        transposes(0, [0])
        transposes(0, [1])
        wg_transposes(0)
        wg_transposes(1)
        regroup(0, [(0, 0), (1, 0)], nc.scalar.copy)
        regroup(0, [(0, 1), (1, 1)], nc.vector.tensor_copy)
        wc_transposes()
        wg_regroup(0, nc.scalar.copy)
        wc_regroup()
        biases()
        quantise_x(0)
        wg_regroup(1, nc.scalar.copy)
        wc_quantise()
        wg_transposes(2)
        wg_transposes(3)
        wg_finish(0)
        transposes(1)
        regroup(1, [(0, 0), (1, 0)], nc.scalar.copy)
        regroup(1, [(0, 1), (1, 1)], nc.vector.tensor_copy)
        stage1(0)
        wg_regroup(2, nc.scalar.copy)
        wg_regroup(3, nc.vector.tensor_copy)
        bias_round(0)
        quantise_x(1)
        wg_finish(1)

        for q in range(1, N_UNITS):
            if has(q + 4, N_UNITS):
                load(q + 4)
            if has(q + 1, N_UNITS):
                transposes(q + 1)
            if has(q - 6, N_BANKS):
                soft_norm(q - 6, [0], nc.vector)
            if has(q - 4, N_BANKS):
                soft_max(q - 4)
                soft_sub(q - 4, nc.gpsimd)
            if has(q - 6, N_BANKS):
                soft_norm(q - 6, [1], nc.vector)
                store(q - 6)
            if has(q - 5, N_BANKS):
                soft_sum(q - 5)
            if has(q - 3, N_BANKS):
                soft_bias(q - 3)
            if has(q - 5, N_BANKS):
                soft_recip(q - 5)
            if has(q + 1, N_UNITS):
                mine = [(1, 1)] if q < 4 else []
                regroup(q + 1, [piece for piece in QUARTERS if piece not in mine], nc.scalar.copy)
                regroup(q + 1, mine, nc.vector.tensor_copy)
            if has(q, N_UNITS):
                stage1(q)
            if has(q - 2, N_BANKS):
                stage2(q - 2)
            if has(q, N_UNITS):
                bias_round(q)
            if has(q + 1, N_UNITS):
                quantise_x(q + 1)
            if has(q - 4, N_BANKS):
                soft_exp(q - 4)
            if q % 2 == 1 and q < N_UNITS - 1:
                quantise_v(q // 2)
            if q == N_UNITS - 1:
                quantise_v(q // 2)
        soft_norm(10, [0, 1], nc.vector)
        store(10)
        stage2(14)
        soft_bias(13)
        stage2(15)
        soft_max(12)
        soft_sub(12, nc.gpsimd)
        soft_exp(12)
        soft_max(13)
        soft_sub(13, nc.gpsimd)
        soft_exp(13)
        soft_sum(11)
        soft_bias(14)
        soft_recip(11)
        soft_bias(15)
        soft_max(14)
        soft_sub(14, nc.gpsimd)
        soft_exp(14)
        soft_norm(11, [0, 1], nc.vector)
        store(11)
        soft_sum(12)
        soft_max(15)
        soft_sub(15, nc.gpsimd)
        soft_exp(15)
        soft_recip(12)
        soft_sum(13)
        soft_norm(12, [0, 1], nc.vector)
        store(12)
        soft_recip(13)
        soft_sum(14)
        soft_norm(13, [0, 1], nc.vector)
        store(13)
        soft_recip(14)
        soft_sum(15)
        soft_norm(14, [0, 1], nc.vector)
        store(14)
        soft_recip(15)
        soft_norm(15, [0, 1], nc.vector)
        store(15)
